import numpy as np
import ml_dtypes


def mxq(x, axis, fmt="e4m3"):
    dtype, down = {"e4m3": (ml_dtypes.float8_e4m3fn, 7), "e5m2": (ml_dtypes.float8_e5m2, 14)}[fmt]
    v = np.moveaxis(np.asarray(x, np.float32).astype(ml_dtypes.bfloat16).astype(np.float64), axis, -1)
    blocks = v.reshape(v.shape[:-1] + (-1, 32))
    amax = np.abs(blocks).max(-1, keepdims=True)
    byte = np.maximum(np.where(amax > 0, np.frexp(amax)[1] - 1 + 127, 0) - down, 1)
    scale = np.exp2(byte - 127.0)
    codes = (blocks / scale).astype(np.float32).astype(dtype).astype(np.float64)
    return np.moveaxis((codes * scale).reshape(v.shape), -1, axis)


WIDE = False


def mx_kscale(k):
    if not WIDE:
        return np.ones(k)
    levels = np.array([10, -10, 5, -5, 0])
    a = np.random.permutation(np.resize(levels, k // 512 * 4)).reshape(k // 512, 4)
    idx = np.arange(k)
    return np.exp2(a[idx // 512, idx % 128 // 32])


BF16 = ml_dtypes.bfloat16


def bf(x):
    return np.asarray(x, np.float32).astype(BF16)


def f64(x):
    return np.asarray(x).astype(np.float64)


B, T, H, P, M = 16, 1024, 1024, 256, 64


def make_mapping():
    m = np.zeros((M, P))
    cols = np.arange(P)
    m[np.random.permutation(cols % M), cols] = 0.5 + np.random.random(P)
    m[np.random.randint(0, M, size=P), cols] = 0.5 + np.random.random(P)
    m[0, 0] = 1.0
    return m


def masked_max(phone, mapping):
    out = np.empty(phone.shape[:2] + (mapping.shape[0],))
    for b in range(phone.shape[0]):
        allo = phone[b][:, None, :] * mapping
        allo = np.where(mapping > 0, allo, -np.inf)
        out[b] = allo.max(-1)
    return out


def log_softmax(v, axis):
    shifted = v - v.max(axis, keepdims=True)
    return shifted - np.log(np.exp(shifted).sum(axis, keepdims=True))


def setup_inputs():
    s = mx_kscale(H)
    return {"enc_output": bf(np.random.standard_normal((B, T, H)) * s),
            "feature2phone": bf(np.random.standard_normal((H, P)) / s[:, None]),
            "mapping": bf(make_mapping())}


def reference(enc_output, feature2phone, mapping):
    mapping = f64(mapping)
    phone = (mxq(f64(enc_output), 2, "e4m3") @ mxq(f64(feature2phone), 0, "e4m3")) / np.sqrt(H)
    phoneme = masked_max(phone, mapping)
    return log_softmax(phoneme, 2)

@@ -1,0 +1,401 @@
+from contextlib import ExitStack
+
+import concourse.mybir as mybir
+from concourse.masks import make_identity
+
+F32 = mybir.dt.float32
+BF16 = mybir.dt.bfloat16
+I32 = mybir.dt.int32
+U32 = mybir.dt.uint32
+U8 = mybir.dt.uint8
+FP8X4 = mybir.dt.float8_e4m3fn_x4
+ALU = mybir.AluOpType
+ACT = mybir.ActivationFunctionType
+AX = mybir.AxisListType
+
+TOKENS = 16 * 1024
+H = 1024
+PHONES = 256
+PHONEMES = 64
+FLOPS = 2 * TOKENS * H * PHONES
+
+P = 128
+BLOCK = 512
+NBLK = TOKENS // BLOCK
+NPAIR = NBLK // 2
+DEPTH = 6
+NV = 2
+CALLS = 2 * NV
+SLOTS = DEPTH * P
+PRE = 12
+PP = PRE // 2
+GROUPS = ((0, 8), (8, 16), (16, 24), (24, 30), (30, 32))
+GROUP_MAX = 8
+F_CALLS = (
+    ((0, 0), (0, 1), (0, 2), (0, 3), (3, 0), (3, 1)),
+    ((1, 0), (1, 1), (1, 2), (1, 3), (3, 2), (3, 3)),
+    ((2, 0), (2, 1), (2, 2), (2, 3)),
+)
+
+
+def tile_compositionalphoneticsmodel_t_kernel(tc, enc_output, feature2phone, mapping, out):
+    nc = tc.nc
+    enc_v = enc_output.rearrange("b t k -> (b t) k").rearrange("(n p s) k -> n p (s k)", p=P, s=4)
+    out_v = out.rearrange("b t m -> (b t) m").rearrange("(n p s) m -> p n (s m)", p=P, s=4)
+    w_v = feature2phone.rearrange("(a q e) p -> e q a p", a=4, q=P, e=2)
+
+    with ExitStack() as ctx:
+        const = ctx.enter_context(tc.tile_pool(name="const", bufs=1))
+        xpool = ctx.enter_context(tc.tile_pool(name="xpool", bufs=4))
+        gpool = ctx.enter_context(tc.tile_pool(name="gpool", bufs=3))
+        cpool = ctx.enter_context(tc.tile_pool(name="cpool", bufs=PRE))
+        apool = ctx.enter_context(tc.tile_pool(name="apool", bufs=4))
+        spool = ctx.enter_context(tc.tile_pool(name="spool", bufs=2))
+        vpool = ctx.enter_context(tc.tile_pool(name="vpool", bufs=2))
+        ps_t = ctx.enter_context(tc.psum_pool(name="ps_t", bufs=2))
+        ps_m = ctx.enter_context(tc.psum_pool(name="ps_m", bufs=3))
+        ps_f = ctx.enter_context(tc.psum_pool(name="ps_f", bufs=1))
+
+        xs = {}
+        grs = {}
+        cds = {}
+        accs = {}
+        pfs = {}
+        m0s = {}
+        vgs = {}
+        grp_of = {}
+        for gi, (g0, g1) in enumerate(GROUPS):
+            for b in range(g0, g1):
+                grp_of[b] = gi
+
+        map2 = const.tile([P, PHONES], BF16)
+        nc.sync.dma_start(out=map2[0:64, :], in_=mapping)
+        nc.sync.dma_start(out=map2[64:128, :], in_=mapping)
+        wl = const.tile([P, 4, 2, PHONES], BF16)
+        for e in range(2):
+            nc.sync.dma_start(out=wl[:, :, e, :], in_=w_v[e])
+
+        def load(b):
+            x = xpool.tile([P, 4 * H], BF16)
+            nc.sync.dma_start(out=x[:], in_=enc_v[b])
+            xs[b] = x
+
+        for b in range(PRE + 2):
+            load(b)
+
+        ident_f = const.tile([P, P], F32)
+        make_identity(nc, ident_f[:])
+        ident_b = const.tile([P, P], BF16)
+        make_identity(nc, ident_b[:])
+        iota_i = const.tile([P, P], I32)
+        nc.gpsimd.iota(iota_i[:], pattern=[[1, P]], base=0, channel_multiplier=0)
+        iota_f = const.tile([P, P], F32)
+        nc.vector.tensor_copy(out=iota_f[:], in_=iota_i[:])
+        part_i = const.tile([P, 1], I32)
+        nc.gpsimd.iota(part_i[:], pattern=[[0, 1]], base=0, channel_multiplier=1)
+        part_f = const.tile([P, 1], F32)
+        nc.vector.tensor_copy(out=part_f[:], in_=part_i[:])
+        slot_i = const.tile([P, NV * DEPTH], I32)
+        nc.gpsimd.iota(slot_i[:], pattern=[[2 * DEPTH, NV], [1, DEPTH]], base=0, channel_multiplier=0)
+        slot_f = const.tile([P, NV * DEPTH], F32)
+        nc.vector.tensor_copy(out=slot_f[:], in_=slot_i[:])
+        half = const.tile([P, 1], F32)
+        nc.vector.tensor_single_scalar(out=half[:], in_=part_f[:], scalar=64.0, op=ALU.is_ge)
+        mcol = const.tile([P, 1], F32)
+        nc.vector.scalar_tensor_tensor(out=mcol[:], in0=half[:], scalar=-64.0, in1=part_f[:], op0=ALU.mult, op1=ALU.add)
+        half_d = const.tile([P, 1], F32)
+        nc.vector.tensor_single_scalar(out=half_d[:], in_=half[:], scalar=float(DEPTH), op=ALU.mult)
+        want0 = const.tile([P, NV * DEPTH], F32)
+        nc.vector.tensor_scalar(out=want0[:], in0=slot_f[:], scalar1=half_d[:, 0:1], scalar2=None, op0=ALU.add)
+        tri = const.tile([P, P], BF16)
+        nc.vector.tensor_scalar(out=tri[:], in0=iota_f[:], scalar1=part_f[:, 0:1], scalar2=None, op0=ALU.is_gt)
+        ones = const.tile([P, P], BF16)
+        nc.vector.memset(ones[:], 1.0)
+        perm4 = const.tile([P, CALLS, P], F32)
+        nc.vector.memset(perm4[:], 0.0)
+        gain_b = const.tile([P, NV, 32], BF16)
+        nc.vector.memset(gain_b[:], 0.0)
+
+        mask = const.tile([P, PHONES], F32)
+        nc.vector.tensor_single_scalar(out=mask[:], in_=map2[:], scalar=0.0, op=ALU.is_gt)
+        incl = const.tile([P, PHONES], F32)
+        nc.vector.tensor_tensor_scan(out=incl[:], data0=mask[:], data1=mask[:], initial=0.0, op0=ALU.add, op1=ALU.max)
+        rank1 = const.tile([P, PHONES], F32)
+        nc.vector.tensor_tensor(out=rank1[:], in0=incl[:], in1=mask[:], op=ALU.mult)
+        count = incl[:, PHONES - 1 : PHONES]
+        valid = const.tile([P, NV * DEPTH], F32)
+        nc.vector.tensor_scalar(out=valid[:], in0=want0[:], scalar1=count, scalar2=None, op0=ALU.is_lt)
+        want_t = const.tile([P, NV * DEPTH], F32)
+        nc.vector.tensor_tensor(out=want_t[:], in0=want0[:], in1=valid[:], op=ALU.mult)
+        want1 = const.tile([P, NV * DEPTH], F32)
+        nc.vector.tensor_single_scalar(out=want1[:], in_=want_t[:], scalar=1.0, op=ALU.add)
+        valid_v = valid[:].rearrange("v (h d) -> v h d", d=DEPTH)
+        active = valid_v[:, :, 0]
+
+        act_b = const.tile([P, NV, 32], BF16)
+        nc.vector.tensor_copy(out=act_b[:], in_=valid_v[:, :, 0:1].to_broadcast([P, NV, 32]))
+        lid_p = ps_m.tile([P, NV, 32], F32, tag="pm")
+        nc.tensor.matmul(out=lid_p[:, 0, :], lhsT=tri[:], rhs=act_b[:, 0, :], start=True, stop=True)
+        nc.tensor.matmul(out=lid_p[:, 1, :], lhsT=ones[:], rhs=act_b[:, 0, :], start=True, stop=False)
+        nc.tensor.matmul(out=lid_p[:, 1, :], lhsT=tri[:], rhs=act_b[:, 1, :], start=False, stop=True)
+        lid_t = const.tile([P, NV], F32)
+        nc.vector.scalar_tensor_tensor(out=lid_t[:], in0=lid_p[:, :, 0], scalar=1.0, in1=active, op0=ALU.add, op1=ALU.mult)
+        lane_id = const.tile([P, NV], F32)
+        nc.vector.tensor_single_scalar(out=lane_id[:], in_=lid_t[:], scalar=-1.0, op=ALU.add)
+        tgt_t = const.tile([P, NV], F32)
+        nc.vector.scalar_tensor_tensor(out=tgt_t[:], in0=lid_p[:, :, 0], scalar=mcol[:, 0:1], in1=active, op0=ALU.subtract, op1=ALU.mult)
+        tgt_b = const.tile([P, NV], BF16)
+        nc.vector.tensor_scalar(out=tgt_b[:], in0=tgt_t[:], scalar1=mcol[:, 0:1], scalar2=None, op0=ALU.add)
+        compact = const.tile([P, NV, P], BF16)
+        for h in range(NV):
+            nc.vector.tensor_scalar(out=compact[:, h, :], in0=iota_f[:], scalar1=lane_id[:, h : h + 1], scalar2=None, op0=ALU.is_equal)
+
+        sel_t = const.tile([P, NV * DEPTH, PHONES], BF16)
+        for d in range(DEPTH):
+            for h in range(NV):
+                j = h * DEPTH + d
+                nc.vector.tensor_scalar(out=sel_t[:, j, :], in0=rank1[:], scalar1=want1[:, j : j + 1], scalar2=None, op0=ALU.is_equal)
+
+        wt = []
+        for c in range(2):
+            wt_p = ps_t.tile([P, 8 * P], BF16, tag="pt")
+            for a in range(4):
+                for e in range(2):
+                    nc.tensor.transpose(wt_p[:, (a * 2 + e) * P : (a * 2 + e + 1) * P], wl[:, a, e, c * P : (c + 1) * P], ident_b[:])
+            wt_c = const.tile([P, 8 * P], BF16, name="wt%d" % c)
+            nc.scalar.copy(out=wt_c[:], in_=wt_p[:])
+            wt.append(wt_c)
+
+        sel = []
+        for c in range(2):
+            sel_c = const.tile([P, SLOTS], BF16, name="sel%d" % c)
+            sel.append(sel_c)
+        for d0, nd in ((0, 4), (4, 2)):
+            for c in range(2):
+                sel_p = ps_m.tile([P, 4 * P], F32, tag="pm")
+                for d in range(d0, d0 + nd):
+                    for h in range(NV):
+                        nc.tensor.matmul(
+                            out=sel_p[:, (d - d0) * P : (d - d0 + 1) * P],
+                            lhsT=sel_t[:, h * DEPTH + d, c * P : (c + 1) * P],
+                            rhs=compact[:, h, :],
+                            start=(h == 0),
+                            stop=(h == NV - 1),
+                        )
+                if c == 0:
+                    nc.vector.tensor_copy(out=sel[c][:, d0 * P : (d0 + nd) * P], in_=sel_p[:, 0 : nd * P])
+                else:
+                    nc.scalar.copy(out=sel[c][:, d0 * P : (d0 + nd) * P], in_=sel_p[:, 0 : nd * P])
+
+        wg = const.tile([P, 2 * SLOTS * 4], BF16, align_bytes=64)
+        w_codes = const.tile([P, 2 * SLOTS], U32, align_bytes=64)
+        w_scales = const.tile([P, 2 * SLOTS], U8, align_bytes=64)
+        for d in range(DEPTH):
+            for g in range(2):
+                wp = ps_m.tile([P, 4 * P], F32, tag="pm")
+                for ue in range(4):
+                    for c in range(2):
+                        nc.tensor.matmul(
+                            out=wp[:, ue * P : (ue + 1) * P],
+                            lhsT=wt[c][:, (g * 4 + ue) * P : (g * 4 + ue + 1) * P],
+                            rhs=sel[c][:, d * P : (d + 1) * P],
+                            start=(c == 0),
+                            stop=(c == 1),
+                        )
+                dst = wg[:, (g * SLOTS + d * P) * 4 : (g * SLOTS + (d + 1) * P) * 4].rearrange("q (l t) -> q l t", t=4)
+                src = wp[:].rearrange("q (t l) -> q l t", t=4)
+                if g == 0:
+                    nc.vector.tensor_copy(out=dst, in_=src)
+                else:
+                    nc.scalar.copy(out=dst, in_=src)
+        for c0, cn in ((0, 512), (512, 256)):
+            for g in range(2):
+                lo = g * SLOTS + c0
+                nc.vector.quantize_mx(
+                    out=w_codes[:, lo : lo + cn].bitcast(FP8X4),
+                    scales=w_scales[:, lo : lo + cn],
+                    in_=wg[:, lo * 4 : (lo + cn) * 4],
+                )
+
+        sg = const.tile([P, NV * DEPTH, PHONES], BF16)
+        nc.vector.tensor_tensor(out=sg[:], in0=sel_t[:], in1=map2[:].unsqueeze(1).to_broadcast([P, NV * DEPTH, PHONES]), op=ALU.mult)
+        gain_v = const.tile([P, NV * DEPTH], F32)
+        nc.vector.tensor_reduce(out=gain_v[:], in_=sg[:], axis=AX.X, op=ALU.add)
+        nc.vector.tensor_copy(out=gain_b[:, :, 0:DEPTH], in_=gain_v[:].rearrange("v (h d) -> v h d", d=DEPTH))
+        gain_p = ps_f.tile([P, 32], F32, tag="pf0")
+        for h in range(NV):
+            nc.tensor.matmul(out=gain_p[:], lhsT=compact[:, h, :], rhs=gain_b[:, h, :], start=(h == 0), stop=(h == NV - 1))
+        gain = const.tile([P, DEPTH], F32)
+        nc.vector.tensor_single_scalar(out=gain[:], in_=gain_p[:, 0:DEPTH], scalar=1.0 / 32.0, op=ALU.mult)
+
+        row_p = ps_f.tile([P, NV * P], F32, tag="pf1")
+        for h in range(NV):
+            nc.tensor.matmul(out=row_p[:, h * P : (h + 1) * P], lhsT=tgt_b[:, h : h + 1].to_broadcast([P, P]), rhs=ident_b[:], start=True, stop=True)
+        nc.vector.tensor_scalar(
+            out=perm4[:, :, 0:64],
+            in0=row_p[:].rearrange("p (i m) -> p i m", m=64),
+            scalar1=part_f[:, 0:1],
+            scalar2=None,
+            op0=ALU.is_equal,
+        )
+
+        neg_max = const.tile([P, NBLK * 4], F32)
+        sums = const.tile([P, NBLK * 4], F32)
+        logs = const.tile([P, NBLK * 4], F32)
+        neg_l = const.tile([P, NBLK * 4], F32)
+
+        def a_bank(b, k):
+            if k == 0:
+                gr = gpool.tile([P, 2 * BLOCK * 4], BF16, align_bytes=64)
+                grs[b] = gr
+            g = k // 2
+            sp = k % 2
+            xw = xs[b][:].bitcast(F32)
+            grw = grs[b][:].bitcast(F32)
+            pt = ps_t.tile([P, 4 * P], F32, tag="pt")
+            for u in range(2):
+                for s2 in range(2):
+                    col = (2 * sp + s2) * 512 + 256 * g + 128 * u
+                    nc.tensor.transpose(pt[:, (u * 2 + s2) * P : (u * 2 + s2 + 1) * P], xw[:, col : col + P], ident_f[:])
+            lo = g * 1024 + sp * 512
+            nc.scalar.copy(
+                out=grw[:, lo : lo + 512].rearrange("q (t u) -> q t u", u=2),
+                in_=pt[:].rearrange("q (u t) -> q t u", u=2),
+            )
+
+        def quant(b):
+            codes = cpool.tile([P, 2 * BLOCK], U32, align_bytes=64)
+            scales = cpool.tile([P, 2 * BLOCK], U8, align_bytes=64)
+            for g in range(2):
+                nc.vector.quantize_mx(
+                    out=codes[:, g * BLOCK : (g + 1) * BLOCK].bitcast(FP8X4),
+                    scales=scales[:, g * BLOCK : (g + 1) * BLOCK],
+                    in_=grs[b][:, g * BLOCK * 4 : (g + 1) * BLOCK * 4],
+                )
+            cds[b] = (codes, scales)
+
+        def mx(b, d):
+            if d == 0:
+                acc = apool.tile([P, BLOCK], F32)
+                accs[b] = acc
+            codes, scales = cds[b]
+            pm = ps_m.tile([P, BLOCK], F32, tag="pm")
+            for g in range(2):
+                lo = g * SLOTS + d * P
+                nc.tensor.matmul_mx(
+                    out=pm[:],
+                    lhsT=w_codes[:, lo : lo + P].bitcast(FP8X4),
+                    lhsT_scale=w_scales[:, lo : lo + P],
+                    rhs=codes[:, g * BLOCK : (g + 1) * BLOCK].bitcast(FP8X4),
+                    rhs_scale=scales[:, g * BLOCK : (g + 1) * BLOCK],
+                    start=(g == 0),
+                    stop=(g == 1),
+                )
+            if d == 0:
+                nc.scalar.activation(out=accs[b][:], in_=pm[:], func=ACT.Copy, scale=gain[:, 0:1])
+            else:
+                nc.vector.scalar_tensor_tensor(out=accs[b][:], in0=pm[:], scalar=gain[:, d : d + 1], in1=accs[b][:], op0=ALU.mult, op1=ALU.max)
+
+        def f_bank(b, k):
+            pf = ps_f.tile([P, 512], F32, tag="pf%d" % k, name="pf%d" % k)
+            for n, (i, s) in enumerate(F_CALLS[k]):
+                nc.tensor.transpose(pf[:, n * 64 : n * 64 + P], accs[b][:, s * P : (s + 1) * P], perm4[:, i, :])
+            pfs[(b, k)] = pf
+            if k == 0:
+                m0 = spool.tile([P, 256], F32)
+                nc.scalar.copy(out=m0[:], in_=pf[:, 0:256])
+                m0s[b] = m0
+
+        def merges(b):
+            gi = grp_of[b]
+            g0 = GROUPS[gi][0]
+            if b == g0:
+                vg = vpool.tile([P, GROUP_MAX * 256], F32)
+                vgs[gi] = vg
+            lo = (b - g0) * 256
+            m1 = spool.tile([P, 256], F32)
+            nc.vector.tensor_tensor(out=m1[:], in0=pfs[(b, 1)][:, 0:256], in1=m0s[b][:], op=ALU.max)
+            m2 = spool.tile([P, 256], F32)
+            nc.vector.tensor_tensor(out=m2[:], in0=pfs[(b, 2)][:, 0:256], in1=m1[:], op=ALU.max)
+            nc.vector.tensor_tensor(out=vgs[gi][:, lo : lo + 128], in0=pfs[(b, 0)][:, 256:384], in1=m2[:, 0:128], op=ALU.max)
+            nc.vector.tensor_tensor(out=vgs[gi][:, lo + 128 : lo + 256], in0=pfs[(b, 1)][:, 256:384], in1=m2[:, 128:256], op=ALU.max)
+            nc.vector.tensor_reduce(
+                out=neg_max[:, b * 4 : (b + 1) * 4],
+                in_=vgs[gi][:, lo : lo + 256].rearrange("p (s m) -> p s m", m=64),
+                axis=AX.X,
+                op=ALU.max,
+                negate=True,
+            )
+
+        def exps(b):
+            gi = grp_of[b]
+            lo = (b - GROUPS[gi][0]) * 256
+            for s in range(4):
+                j = b * 4 + s
+                ex = spool.tile([P, 64], F32)
+                nc.scalar.activation(
+                    out=ex[:],
+                    in_=vgs[gi][:, lo + s * 64 : lo + (s + 1) * 64],
+                    func=ACT.Exp,
+                    bias=neg_max[:, j : j + 1],
+                    scale=1.0,
+                    accum_out=sums[:, j : j + 1],
+                )
+
+        def group_end(gi):
+            g0, g1 = GROUPS[gi]
+            n = (g1 - g0) * 4
+            cols = slice(g0 * 4, g1 * 4)
+            last = gi == len(GROUPS) - 1
+            eng = nc.vector if last else nc.gpsimd
+            queue = nc.sync if last else nc.gpsimd
+            nc.scalar.activation(out=logs[:, cols], in_=sums[:, cols], func=ACT.Ln)
+            eng.tensor_tensor(out=neg_l[:, cols], in0=neg_max[:, cols], in1=logs[:, cols], op=ALU.subtract)
+            vg = vgs[gi][:, 0 : n * 64]
+            vg3 = vg.rearrange("p (j m) -> p j m", m=64)
+            eng.tensor_tensor(out=vg3, in0=vg3, in1=neg_l[:, cols].unsqueeze(2).to_broadcast([P, n, 64]), op=ALU.add)
+            queue.dma_start(out=out_v[:, g0:g1, :], in_=vg.rearrange("p (n f) -> p n f", f=256))
+
+        for b in range(PRE):
+            for k in range(4):
+                a_bank(b, k)
+            if b >= 1 and b - 1 < PRE - 2:
+                quant(b - 1)
+
+        with tc.manual_schedule():
+            for j in range(NPAIR + 2):
+                for b in (2 * (j + PP + 1), 2 * (j + PP + 1) + 1):
+                    if b < NBLK:
+                        load(b)
+                for d in range(DEPTH):
+                    if j < NPAIR:
+                        mx(2 * j, d)
+                        mx(2 * j + 1, d)
+                    if d == 0 and j >= 2:
+                        exps(2 * (j - 2))
+                        exps(2 * (j - 2) + 1)
+                        for gi in range(len(GROUPS)):
+                            if GROUPS[gi][1] == 2 * (j - 1):
+                                group_end(gi)
+                for idx in range(2):
+                    c = 2 * (j + PP) + idx
+                    p = 2 * (j - 1) + idx
+                    q = 2 * (j + PP - 1) + idx
+                    has_a = c < NBLK
+                    has_f = 0 <= p < NBLK
+                    if q < NBLK:
+                        quant(q)
+                    if has_a:
+                        a_bank(c, 0)
+                        a_bank(c, 1)
+                    if has_f:
+                        f_bank(p, 0)
+                    if has_a:
+                        a_bank(c, 2)
+                    if has_f:
+                        f_bank(p, 1)
+                    if has_a:
+                        a_bank(c, 3)
+                    if has_f:
+                        f_bank(p, 2)
+                        merges(p)

@@ -25,17 +25,13 @@ NBLK = TOKENS // BLOCK
 NPAIR = NBLK // 2
 DEPTH = 6
 NV = 2
-CALLS = 2 * NV
 SLOTS = DEPTH * P
-PRE = 12
-PP = PRE // 2
-GROUPS = ((0, 8), (8, 16), (16, 24), (24, 30), (30, 32))
-GROUP_MAX = 8
-F_CALLS = (
-    ((0, 0), (0, 1), (0, 2), (0, 3), (3, 0), (3, 1)),
-    ((1, 0), (1, 1), (1, 2), (1, 3), (3, 2), (3, 3)),
-    ((2, 0), (2, 1), (2, 2), (2, 3)),
-)
+AHEAD = 3
+GROUPS = ((0, 12), (12, 22), (22, 28), (28, 32))
+NEG_BIG = -3.0e38
+W_ENG = ("sv", "sv", "sv", "sv", "sv", "sv")
+EARLY_N = (2, 2, 3, 3, 3, 3)
+EARLY_ENG = ("s", "s", "s", "s", "s", "s")
 
 
 def tile_compositionalphoneticsmodel_t_kernel(tc, enc_output, feature2phone, mapping, out):
@@ -47,26 +43,23 @@ def tile_compositionalphoneticsmodel_t_kernel(tc, enc_output, feature2phone, map
     with ExitStack() as ctx:
         const = ctx.enter_context(tc.tile_pool(name="const", bufs=1))
         xpool = ctx.enter_context(tc.tile_pool(name="xpool", bufs=4))
-        gpool = ctx.enter_context(tc.tile_pool(name="gpool", bufs=3))
-        cpool = ctx.enter_context(tc.tile_pool(name="cpool", bufs=PRE))
-        apool = ctx.enter_context(tc.tile_pool(name="apool", bufs=4))
+        gpool = ctx.enter_context(tc.tile_pool(name="gpool", bufs=4))
+        cpool = ctx.enter_context(tc.tile_pool(name="cpool", bufs=8))
+        apool = ctx.enter_context(tc.tile_pool(name="apool", bufs=6))
         spool = ctx.enter_context(tc.tile_pool(name="spool", bufs=2))
-        vpool = ctx.enter_context(tc.tile_pool(name="vpool", bufs=2))
-        ps_t = ctx.enter_context(tc.psum_pool(name="ps_t", bufs=2))
+        ps_t = ctx.enter_context(tc.psum_pool(name="ps_t", bufs=3))
         ps_m = ctx.enter_context(tc.psum_pool(name="ps_m", bufs=3))
         ps_f = ctx.enter_context(tc.psum_pool(name="ps_f", bufs=1))
+        ctx.enter_context(tc.manual_schedule())
 
         xs = {}
         grs = {}
         cds = {}
         accs = {}
         pfs = {}
-        m0s = {}
-        vgs = {}
-        grp_of = {}
-        for gi, (g0, g1) in enumerate(GROUPS):
-            for b in range(g0, g1):
-                grp_of[b] = gi
+        c0s = {}
+        tps = {}
+        t3s = {}
 
         map2 = const.tile([P, PHONES], BF16)
         nc.sync.dma_start(out=map2[0:64, :], in_=mapping)
@@ -80,39 +73,34 @@ def tile_compositionalphoneticsmodel_t_kernel(tc, enc_output, feature2phone, map
             nc.sync.dma_start(out=x[:], in_=enc_v[b])
             xs[b] = x
 
-        for b in range(PRE + 2):
+        for b in range(4):
             load(b)
 
-        ident_f = const.tile([P, P], F32)
-        make_identity(nc, ident_f[:])
-        ident_b = const.tile([P, P], BF16)
-        make_identity(nc, ident_b[:])
-        iota_i = const.tile([P, P], I32)
-        nc.gpsimd.iota(iota_i[:], pattern=[[1, P]], base=0, channel_multiplier=0)
-        iota_f = const.tile([P, P], F32)
-        nc.vector.tensor_copy(out=iota_f[:], in_=iota_i[:])
         part_i = const.tile([P, 1], I32)
         nc.gpsimd.iota(part_i[:], pattern=[[0, 1]], base=0, channel_multiplier=1)
-        part_f = const.tile([P, 1], F32)
-        nc.vector.tensor_copy(out=part_f[:], in_=part_i[:])
         slot_i = const.tile([P, NV * DEPTH], I32)
         nc.gpsimd.iota(slot_i[:], pattern=[[2 * DEPTH, NV], [1, DEPTH]], base=0, channel_multiplier=0)
+        iota_i = const.tile([P, P], I32)
+        nc.gpsimd.iota(iota_i[:], pattern=[[1, P]], base=0, channel_multiplier=0)
+        ident_b = const.tile([P, P], BF16)
+        make_identity(nc, ident_b[:])
+        ident_f = const.tile([P, P], F32)
+        make_identity(nc, ident_f[:])
+
+        part_f = const.tile([P, 1], F32)
+        nc.vector.tensor_copy(out=part_f[:], in_=part_i[:])
         slot_f = const.tile([P, NV * DEPTH], F32)
         nc.vector.tensor_copy(out=slot_f[:], in_=slot_i[:])
-        half = const.tile([P, 1], F32)
-        nc.vector.tensor_single_scalar(out=half[:], in_=part_f[:], scalar=64.0, op=ALU.is_ge)
-        mcol = const.tile([P, 1], F32)
-        nc.vector.scalar_tensor_tensor(out=mcol[:], in0=half[:], scalar=-64.0, in1=part_f[:], op0=ALU.mult, op1=ALU.add)
         half_d = const.tile([P, 1], F32)
-        nc.vector.tensor_single_scalar(out=half_d[:], in_=half[:], scalar=float(DEPTH), op=ALU.mult)
+        nc.vector.tensor_scalar(out=half_d[:], in0=part_f[:], scalar1=64.0, scalar2=float(DEPTH), op0=ALU.is_ge, op1=ALU.mult)
         want0 = const.tile([P, NV * DEPTH], F32)
         nc.vector.tensor_scalar(out=want0[:], in0=slot_f[:], scalar1=half_d[:, 0:1], scalar2=None, op0=ALU.add)
+        iota_f = const.tile([P, P], F32)
+        nc.vector.tensor_copy(out=iota_f[:], in_=iota_i[:])
         tri = const.tile([P, P], BF16)
         nc.vector.tensor_scalar(out=tri[:], in0=iota_f[:], scalar1=part_f[:, 0:1], scalar2=None, op0=ALU.is_gt)
         ones = const.tile([P, P], BF16)
         nc.vector.memset(ones[:], 1.0)
-        perm4 = const.tile([P, CALLS, P], F32)
-        nc.vector.memset(perm4[:], 0.0)
         gain_b = const.tile([P, NV, 32], BF16)
         nc.vector.memset(gain_b[:], 0.0)
 
@@ -125,39 +113,49 @@ def tile_compositionalphoneticsmodel_t_kernel(tc, enc_output, feature2phone, map
         count = incl[:, PHONES - 1 : PHONES]
         valid = const.tile([P, NV * DEPTH], F32)
         nc.vector.tensor_scalar(out=valid[:], in0=want0[:], scalar1=count, scalar2=None, op0=ALU.is_lt)
+        valid_v = valid[:].rearrange("v (h d) -> v h d", d=DEPTH)
+        active = valid_v[:, :, 0]
+        act_b = const.tile([P, NV, 32], BF16)
+        nc.vector.tensor_copy(out=act_b[:], in_=valid_v[:, :, 0:1].to_broadcast([P, NV, 32]))
         want_t = const.tile([P, NV * DEPTH], F32)
         nc.vector.tensor_tensor(out=want_t[:], in0=want0[:], in1=valid[:], op=ALU.mult)
         want1 = const.tile([P, NV * DEPTH], F32)
         nc.vector.tensor_single_scalar(out=want1[:], in_=want_t[:], scalar=1.0, op=ALU.add)
-        valid_v = valid[:].rearrange("v (h d) -> v h d", d=DEPTH)
-        active = valid_v[:, :, 0]
 
-        act_b = const.tile([P, NV, 32], BF16)
-        nc.vector.tensor_copy(out=act_b[:], in_=valid_v[:, :, 0:1].to_broadcast([P, NV, 32]))
         lid_p = ps_m.tile([P, NV, 32], F32, tag="pm")
         nc.tensor.matmul(out=lid_p[:, 0, :], lhsT=tri[:], rhs=act_b[:, 0, :], start=True, stop=True)
         nc.tensor.matmul(out=lid_p[:, 1, :], lhsT=ones[:], rhs=act_b[:, 0, :], start=True, stop=False)
         nc.tensor.matmul(out=lid_p[:, 1, :], lhsT=tri[:], rhs=act_b[:, 1, :], start=False, stop=True)
+
+        sgw = const.tile([P, NV * DEPTH, PHONES], BF16)
+        gain_v = const.tile([P, NV * DEPTH], F32)
+
+        def sgw_make(d):
+            for h in range(NV):
+                j = h * DEPTH + d
+                nc.vector.scalar_tensor_tensor(
+                    out=sgw[:, j, :], in0=rank1[:], scalar=want1[:, j : j + 1], in1=map2[:],
+                    op0=ALU.is_equal, op1=ALU.mult, accum_out=gain_v[:, j : j + 1],
+                )
+
+        sgw_make(0)
+
         lid_t = const.tile([P, NV], F32)
         nc.vector.scalar_tensor_tensor(out=lid_t[:], in0=lid_p[:, :, 0], scalar=1.0, in1=active, op0=ALU.add, op1=ALU.mult)
         lane_id = const.tile([P, NV], F32)
         nc.vector.tensor_single_scalar(out=lane_id[:], in_=lid_t[:], scalar=-1.0, op=ALU.add)
-        tgt_t = const.tile([P, NV], F32)
-        nc.vector.scalar_tensor_tensor(out=tgt_t[:], in0=lid_p[:, :, 0], scalar=mcol[:, 0:1], in1=active, op0=ALU.subtract, op1=ALU.mult)
-        tgt_b = const.tile([P, NV], BF16)
-        nc.vector.tensor_scalar(out=tgt_b[:], in0=tgt_t[:], scalar1=mcol[:, 0:1], scalar2=None, op0=ALU.add)
         compact = const.tile([P, NV, P], BF16)
         for h in range(NV):
             nc.vector.tensor_scalar(out=compact[:, h, :], in0=iota_f[:], scalar1=lane_id[:, h : h + 1], scalar2=None, op0=ALU.is_equal)
-
-        sel_t = const.tile([P, NV * DEPTH, PHONES], BF16)
-        for d in range(DEPTH):
-            for h in range(NV):
-                j = h * DEPTH + d
-                nc.vector.tensor_scalar(out=sel_t[:, j, :], in0=rank1[:], scalar1=want1[:, j : j + 1], scalar2=None, op0=ALU.is_equal)
+        tg1 = const.tile([P, 1], F32)
+        nc.vector.scalar_tensor_tensor(out=tg1[:], in0=lid_p[:, 1, 0:1], scalar=lane_id[:, 0:1], in1=valid_v[:, 1, 0:1], op0=ALU.subtract, op1=ALU.mult)
+        tgt_b = const.tile([P, NV], BF16)
+        nc.vector.tensor_copy(out=tgt_b[:, 0:1], in_=lane_id[:, 0:1])
+        nc.vector.tensor_scalar(out=tgt_b[:, 1:2], in0=tg1[:], scalar1=lane_id[:, 0:1], scalar2=None, op0=ALU.add)
 
         wt = []
-        for c in range(2):
+
+        def wt_make(c):
             wt_p = ps_t.tile([P, 8 * P], BF16, tag="pt")
             for a in range(4):
                 for e in range(2):
@@ -166,31 +164,26 @@ def tile_compositionalphoneticsmodel_t_kernel(tc, enc_output, feature2phone, map
             nc.scalar.copy(out=wt_c[:], in_=wt_p[:])
             wt.append(wt_c)
 
-        sel = []
-        for c in range(2):
-            sel_c = const.tile([P, SLOTS], BF16, name="sel%d" % c)
-            sel.append(sel_c)
-        for d0, nd in ((0, 4), (4, 2)):
-            for c in range(2):
-                sel_p = ps_m.tile([P, 4 * P], F32, tag="pm")
-                for d in range(d0, d0 + nd):
-                    for h in range(NV):
-                        nc.tensor.matmul(
-                            out=sel_p[:, (d - d0) * P : (d - d0 + 1) * P],
-                            lhsT=sel_t[:, h * DEPTH + d, c * P : (c + 1) * P],
-                            rhs=compact[:, h, :],
-                            start=(h == 0),
-                            stop=(h == NV - 1),
-                        )
-                if c == 0:
-                    nc.vector.tensor_copy(out=sel[c][:, d0 * P : (d0 + nd) * P], in_=sel_p[:, 0 : nd * P])
-                else:
-                    nc.scalar.copy(out=sel[c][:, d0 * P : (d0 + nd) * P], in_=sel_p[:, 0 : nd * P])
+        sel = const.tile([P, DEPTH, 2, P], BF16)
 
-        wg = const.tile([P, 2 * SLOTS * 4], BF16, align_bytes=64)
-        w_codes = const.tile([P, 2 * SLOTS], U32, align_bytes=64)
-        w_scales = const.tile([P, 2 * SLOTS], U8, align_bytes=64)
-        for d in range(DEPTH):
+        def sel_make(d):
+            sel_p = ps_f.tile([P, 2, P], F32, tag="pf%d" % (d % 2), name="sel_p")
+            for c in range(2):
+                for h in range(NV):
+                    nc.tensor.matmul(
+                        out=sel_p[:, c, :],
+                        lhsT=sgw[:, h * DEPTH + d, c * P : (c + 1) * P],
+                        rhs=compact[:, h, :],
+                        start=(h == 0),
+                        stop=(h == NV - 1),
+                    )
+            nc.scalar.activation(out=sel[:, d, :, :], in_=sel_p[:], func=ACT.Sign)
+
+        wg = const.tile([P, 2, DEPTH, P * 4], BF16, align_bytes=64)
+        w_codes = const.tile([P, 2, DEPTH, P], U32, align_bytes=64)
+        w_scales = const.tile([P, 2, DEPTH, P], U8, align_bytes=64)
+
+        def wslot_make(d, engines):
             for g in range(2):
                 wp = ps_m.tile([P, 4 * P], F32, tag="pm")
                 for ue in range(4):
@@ -198,53 +191,46 @@ def tile_compositionalphoneticsmodel_t_kernel(tc, enc_output, feature2phone, map
                         nc.tensor.matmul(
                             out=wp[:, ue * P : (ue + 1) * P],
                             lhsT=wt[c][:, (g * 4 + ue) * P : (g * 4 + ue + 1) * P],
-                            rhs=sel[c][:, d * P : (d + 1) * P],
+                            rhs=sel[:, d, c, :],
                             start=(c == 0),
                             stop=(c == 1),
                         )
-                dst = wg[:, (g * SLOTS + d * P) * 4 : (g * SLOTS + (d + 1) * P) * 4].rearrange("q (l t) -> q l t", t=4)
+                dst = wg[:, g, d, :].rearrange("q (l t) -> q l t", t=4)
                 src = wp[:].rearrange("q (t l) -> q l t", t=4)
-                if g == 0:
+                if engines[g] == "v":
                     nc.vector.tensor_copy(out=dst, in_=src)
                 else:
                     nc.scalar.copy(out=dst, in_=src)
-        for c0, cn in ((0, 512), (512, 256)):
+
+        def wslot_quant(d):
             for g in range(2):
-                lo = g * SLOTS + c0
-                nc.vector.quantize_mx(
-                    out=w_codes[:, lo : lo + cn].bitcast(FP8X4),
-                    scales=w_scales[:, lo : lo + cn],
-                    in_=wg[:, lo * 4 : (lo + cn) * 4],
-                )
+                nc.vector.quantize_mx(out=w_codes[:, g, d, :].bitcast(FP8X4), scales=w_scales[:, g, d, :], in_=wg[:, g, d, :])
 
-        sg = const.tile([P, NV * DEPTH, PHONES], BF16)
-        nc.vector.tensor_tensor(out=sg[:], in0=sel_t[:], in1=map2[:].unsqueeze(1).to_broadcast([P, NV * DEPTH, PHONES]), op=ALU.mult)
-        gain_v = const.tile([P, NV * DEPTH], F32)
-        nc.vector.tensor_reduce(out=gain_v[:], in_=sg[:], axis=AX.X, op=ALU.add)
-        nc.vector.tensor_copy(out=gain_b[:, :, 0:DEPTH], in_=gain_v[:].rearrange("v (h d) -> v h d", d=DEPTH))
-        gain_p = ps_f.tile([P, 32], F32, tag="pf0")
-        for h in range(NV):
-            nc.tensor.matmul(out=gain_p[:], lhsT=compact[:, h, :], rhs=gain_b[:, h, :], start=(h == 0), stop=(h == NV - 1))
         gain = const.tile([P, DEPTH], F32)
-        nc.vector.tensor_single_scalar(out=gain[:], in_=gain_p[:, 0:DEPTH], scalar=1.0 / 32.0, op=ALU.mult)
+        perm2 = const.tile([P, NV * P], F32)
+        bias = const.tile([P, PHONEMES], F32)
 
-        row_p = ps_f.tile([P, NV * P], F32, tag="pf1")
-        for h in range(NV):
-            nc.tensor.matmul(out=row_p[:, h * P : (h + 1) * P], lhsT=tgt_b[:, h : h + 1].to_broadcast([P, P]), rhs=ident_b[:], start=True, stop=True)
-        nc.vector.tensor_scalar(
-            out=perm4[:, :, 0:64],
-            in0=row_p[:].rearrange("p (i m) -> p i m", m=64),
-            scalar1=part_f[:, 0:1],
-            scalar2=None,
-            op0=ALU.is_equal,
-        )
+        def gain_make():
+            nc.vector.tensor_copy(out=gain_b[:, :, 0:DEPTH], in_=gain_v[:].rearrange("v (h d) -> v h d", d=DEPTH))
+            gain_p = ps_f.tile([P, 32], F32, tag="pf0")
+            for h in range(NV):
+                nc.tensor.matmul(out=gain_p[:], lhsT=compact[:, h, :], rhs=gain_b[:, h, :], start=(h == 0), stop=(h == NV - 1))
+            nc.vector.tensor_single_scalar(out=gain[:], in_=gain_p[:, 0:DEPTH], scalar=1.0 / 32.0, op=ALU.mult)
 
+        def perm_make():
+            row_p = ps_f.tile([P, NV * P], F32, tag="pf1")
+            for h in range(NV):
+                nc.tensor.matmul(out=row_p[:, h * P : (h + 1) * P], lhsT=tgt_b[:, h : h + 1].to_broadcast([P, P]), rhs=ident_b[:], start=True, stop=True)
+            nc.vector.tensor_scalar(out=perm2[:], in0=row_p[:], scalar1=part_f[:, 0:1], scalar2=None, op0=ALU.is_equal)
+            nc.vector.tensor_scalar(out=bias[:], in0=row_p[:, 64:128], scalar1=0.0, scalar2=NEG_BIG, op0=ALU.is_lt, op1=ALU.mult)
+
+        v_all = const.tile([P, NBLK * 256], F32)
         neg_max = const.tile([P, NBLK * 4], F32)
         sums = const.tile([P, NBLK * 4], F32)
         logs = const.tile([P, NBLK * 4], F32)
         neg_l = const.tile([P, NBLK * 4], F32)
 
-        def a_bank(b, k):
+        def a_bank(b, k, engine="s"):
             if k == 0:
                 gr = gpool.tile([P, 2 * BLOCK * 4], BF16, align_bytes=64)
                 grs[b] = gr
@@ -258,21 +244,24 @@ def tile_compositionalphoneticsmodel_t_kernel(tc, enc_output, feature2phone, map
                     col = (2 * sp + s2) * 512 + 256 * g + 128 * u
                     nc.tensor.transpose(pt[:, (u * 2 + s2) * P : (u * 2 + s2 + 1) * P], xw[:, col : col + P], ident_f[:])
             lo = g * 1024 + sp * 512
-            nc.scalar.copy(
-                out=grw[:, lo : lo + 512].rearrange("q (t u) -> q t u", u=2),
-                in_=pt[:].rearrange("q (u t) -> q t u", u=2),
-            )
+            dst = grw[:, lo : lo + 512].rearrange("q (t u) -> q t u", u=2)
+            src = pt[:].rearrange("q (u t) -> q t u", u=2)
+            if engine == "v":
+                nc.vector.tensor_copy(out=dst, in_=src)
+            else:
+                nc.scalar.copy(out=dst, in_=src)
 
-        def quant(b):
-            codes = cpool.tile([P, 2 * BLOCK], U32, align_bytes=64)
-            scales = cpool.tile([P, 2 * BLOCK], U8, align_bytes=64)
-            for g in range(2):
-                nc.vector.quantize_mx(
-                    out=codes[:, g * BLOCK : (g + 1) * BLOCK].bitcast(FP8X4),
-                    scales=scales[:, g * BLOCK : (g + 1) * BLOCK],
-                    in_=grs[b][:, g * BLOCK * 4 : (g + 1) * BLOCK * 4],
-                )
-            cds[b] = (codes, scales)
+        def quant(b, g):
+            if g == 0:
+                codes = cpool.tile([P, 2 * BLOCK], U32, align_bytes=64)
+                scales = cpool.tile([P, 2 * BLOCK], U8, align_bytes=64)
+                cds[b] = (codes, scales)
+            codes, scales = cds[b]
+            nc.vector.quantize_mx(
+                out=codes[:, g * BLOCK : (g + 1) * BLOCK].bitcast(FP8X4),
+                scales=scales[:, g * BLOCK : (g + 1) * BLOCK],
+                in_=grs[b][:, g * BLOCK * 4 : (g + 1) * BLOCK * 4],
+            )
 
         def mx(b, d):
             if d == 0:
@@ -281,11 +270,10 @@ def tile_compositionalphoneticsmodel_t_kernel(tc, enc_output, feature2phone, map
             codes, scales = cds[b]
             pm = ps_m.tile([P, BLOCK], F32, tag="pm")
             for g in range(2):
-                lo = g * SLOTS + d * P
                 nc.tensor.matmul_mx(
                     out=pm[:],
-                    lhsT=w_codes[:, lo : lo + P].bitcast(FP8X4),
-                    lhsT_scale=w_scales[:, lo : lo + P],
+                    lhsT=w_codes[:, g, d, :].bitcast(FP8X4),
+                    lhsT_scale=w_scales[:, g, d, :],
                     rhs=codes[:, g * BLOCK : (g + 1) * BLOCK].bitcast(FP8X4),
                     rhs_scale=scales[:, g * BLOCK : (g + 1) * BLOCK],
                     start=(g == 0),
@@ -296,106 +284,148 @@ def tile_compositionalphoneticsmodel_t_kernel(tc, enc_output, feature2phone, map
             else:
                 nc.vector.scalar_tensor_tensor(out=accs[b][:], in0=pm[:], scalar=gain[:, d : d + 1], in1=accs[b][:], op0=ALU.mult, op1=ALU.max)
 
-        def f_bank(b, k):
-            pf = ps_f.tile([P, 512], F32, tag="pf%d" % k, name="pf%d" % k)
-            for n, (i, s) in enumerate(F_CALLS[k]):
-                nc.tensor.transpose(pf[:, n * 64 : n * 64 + P], accs[b][:, s * P : (s + 1) * P], perm4[:, i, :])
-            pfs[(b, k)] = pf
-            if k == 0:
-                m0 = spool.tile([P, 256], F32)
-                nc.scalar.copy(out=m0[:], in_=pf[:, 0:256])
-                m0s[b] = m0
+        def f_bank(b, h):
+            pf = ps_f.tile([P, 4 * P], F32, tag="pf%d" % h, name="pf%d" % h)
+            for s in range(4):
+                nc.tensor.transpose(pf[:, s * P : (s + 1) * P], accs[b][:, s * P : (s + 1) * P], perm2[:, h * P : (h + 1) * P])
+            pfs[(b, h)] = pf
+            if h == 0:
+                c0 = spool.tile([P, 4 * P], F32)
+                nc.scalar.copy(out=c0[:], in_=pf[:])
+                c0s[b] = c0
 
-        def merges(b):
-            gi = grp_of[b]
-            g0 = GROUPS[gi][0]
-            if b == g0:
-                vg = vpool.tile([P, GROUP_MAX * 256], F32)
-                vgs[gi] = vg
-            lo = (b - g0) * 256
-            m1 = spool.tile([P, 256], F32)
-            nc.vector.tensor_tensor(out=m1[:], in0=pfs[(b, 1)][:, 0:256], in1=m0s[b][:], op=ALU.max)
-            m2 = spool.tile([P, 256], F32)
-            nc.vector.tensor_tensor(out=m2[:], in0=pfs[(b, 2)][:, 0:256], in1=m1[:], op=ALU.max)
-            nc.vector.tensor_tensor(out=vgs[gi][:, lo : lo + 128], in0=pfs[(b, 0)][:, 256:384], in1=m2[:, 0:128], op=ALU.max)
-            nc.vector.tensor_tensor(out=vgs[gi][:, lo + 128 : lo + 256], in0=pfs[(b, 1)][:, 256:384], in1=m2[:, 128:256], op=ALU.max)
-            nc.vector.tensor_reduce(
-                out=neg_max[:, b * 4 : (b + 1) * 4],
-                in_=vgs[gi][:, lo : lo + 256].rearrange("p (s m) -> p s m", m=64),
-                axis=AX.X,
-                op=ALU.max,
-                negate=True,
+        def t_max(b):
+            if b % 2 == 0:
+                tp = spool.tile([P, 2, 4, P], F32)
+                tps[b // 2] = tp
+            nc.vector.tensor_tensor(out=tps[b // 2][:, b % 2, :, :].rearrange("p s c -> p (s c)"), in0=pfs[(b, 1)][:], in1=c0s[b][:], op=ALU.max)
+
+        def bias_add(j, eng):
+            t3 = spool.tile([P, 8, PHONEMES], F32)
+            t3s[j] = t3
+            eng.tensor_tensor(
+                out=t3[:],
+                in0=tps[j][:].rearrange("p b s c -> p (b s) c")[:, :, 64:128],
+                in1=bias[:].unsqueeze(1).to_broadcast([P, 8, PHONEMES]),
+                op=ALU.add,
             )
 
-        def exps(b):
-            gi = grp_of[b]
-            lo = (b - GROUPS[gi][0]) * 256
-            for s in range(4):
-                j = b * 4 + s
-                ex = spool.tile([P, 64], F32)
+        def v_max(j):
+            vv = v_all[:, j * 512 : (j + 1) * 512].rearrange("p (s m) -> p s m", m=PHONEMES)
+            nc.vector.tensor_tensor(out=vv, in0=tps[j][:].rearrange("p b s c -> p (b s) c")[:, :, 0:64], in1=t3s[j][:], op=ALU.max)
+            nc.vector.tensor_reduce(out=neg_max[:, j * 8 : (j + 1) * 8], in_=vv, axis=AX.X, op=ALU.max, negate=True)
+
+        def exps(j):
+            for i in range(j * 8, j * 8 + 8):
+                ex = spool.tile([P, PHONEMES], F32)
                 nc.scalar.activation(
-                    out=ex[:],
-                    in_=vgs[gi][:, lo + s * 64 : lo + (s + 1) * 64],
-                    func=ACT.Exp,
-                    bias=neg_max[:, j : j + 1],
-                    scale=1.0,
-                    accum_out=sums[:, j : j + 1],
+                    out=ex[:], in_=v_all[:, i * 64 : (i + 1) * 64], func=ACT.Exp,
+                    bias=neg_max[:, i : i + 1], scale=1.0, accum_out=sums[:, i : i + 1],
                 )
 
-        def group_end(gi):
+        def group_ln(gi, eng):
             g0, g1 = GROUPS[gi]
-            n = (g1 - g0) * 4
             cols = slice(g0 * 4, g1 * 4)
-            last = gi == len(GROUPS) - 1
-            eng = nc.vector if last else nc.gpsimd
-            queue = nc.sync if last else nc.gpsimd
             nc.scalar.activation(out=logs[:, cols], in_=sums[:, cols], func=ACT.Ln)
             eng.tensor_tensor(out=neg_l[:, cols], in0=neg_max[:, cols], in1=logs[:, cols], op=ALU.subtract)
-            vg = vgs[gi][:, 0 : n * 64]
-            vg3 = vg.rearrange("p (j m) -> p j m", m=64)
-            eng.tensor_tensor(out=vg3, in0=vg3, in1=neg_l[:, cols].unsqueeze(2).to_broadcast([P, n, 64]), op=ALU.add)
-            queue.dma_start(out=out_v[:, g0:g1, :], in_=vg.rearrange("p (n f) -> p n f", f=256))
 
-        for b in range(PRE):
-            for k in range(4):
-                a_bank(b, k)
-            if b >= 1 and b - 1 < PRE - 2:
-                quant(b - 1)
+        def finish(b0, b1, eng, queue):
+            n = (b1 - b0) * 4
+            vg = v_all[:, b0 * 256 : b1 * 256]
+            vg3 = vg.rearrange("p (i m) -> p i m", m=PHONEMES)
+            eng.tensor_tensor(out=vg3, in0=vg3, in1=neg_l[:, b0 * 4 : b1 * 4].unsqueeze(2).to_broadcast([P, n, PHONEMES]), op=ALU.add)
+            queue.dma_start(out=out_v[:, b0:b1, :], in_=vg.rearrange("p (n f) -> p n f", f=256))
 
-        with tc.manual_schedule():
-            for j in range(NPAIR + 2):
-                for b in (2 * (j + PP + 1), 2 * (j + PP + 1) + 1):
-                    if b < NBLK:
-                        load(b)
-                for d in range(DEPTH):
+        def a_block(b, ks, engine="s"):
+            for k in ks:
+                a_bank(b, k, engine)
+                if k == 3 and b + 4 < NBLK:
+                    load(b + 4)
+
+        wt_make(0)
+        wt_make(1)
+        sel_make(0)
+        sgw_make(1)
+        sel_make(1)
+        sgw_make(2)
+        early = [(b, k) for b in range(4) for k in range(4)]
+        for d in range(DEPTH):
+            wslot_make(d, W_ENG[d])
+            if d + 2 < DEPTH:
+                sel_make(d + 2)
+            if d + 3 < DEPTH:
+                sgw_make(d + 3)
+            for b, k in early[sum(EARLY_N[:d]) : sum(EARLY_N[: d + 1])]:
+                a_block(b, [k], EARLY_ENG[d])
+            wslot_quant(d)
+            if d == 3:
+                quant(0, 0)
+                quant(0, 1)
+            if d == 4:
+                gain_make()
+                perm_make()
+        for b, k in early[sum(EARLY_N) :]:
+            a_block(b, [k])
+        quant(1, 0)
+        quant(1, 1)
+        mx(0, 0)
+        mx(1, 0)
+        quant(2, 0)
+        quant(2, 1)
+        quant(3, 0)
+        quant(3, 1)
+
+        pending = []
+        finished = 0
+        for j in range(NPAIR + 2):
+            p0, p1 = 2 * j, 2 * j + 1
+            n0, n1 = p0 + 2, p1 + 2
+            if j == 0:
+                a_list = [[4, 5], [6, 7]]
+                q_list = [[], [4, 5]]
+            else:
+                a_list = [[b] if b < NBLK else [] for b in (p0 + 2 * AHEAD, p1 + 2 * AHEAD)]
+                q_list = [[b] if b < NBLK else [] for b in (p0 + 2 * AHEAD - 2, p1 + 2 * AHEAD - 2)]
+            f_list = [p0 - 2, p1 - 2] if 1 <= j <= NPAIR else []
+            for half in range(2):
+                if half == 0:
                     if j < NPAIR:
-                        mx(2 * j, d)
-                        mx(2 * j + 1, d)
-                    if d == 0 and j >= 2:
-                        exps(2 * (j - 2))
-                        exps(2 * (j - 2) + 1)
+                        for d in (1, 2):
+                            mx(p0, d)
+                            mx(p1, d)
+                    if n0 < NBLK:
+                        mx(n0, 0)
+                        mx(n1, 0)
+                    if j >= 2:
+                        v_max(j - 2)
+                else:
+                    if j >= 2:
+                        exps(j - 2)
                         for gi in range(len(GROUPS)):
                             if GROUPS[gi][1] == 2 * (j - 1):
-                                group_end(gi)
-                for idx in range(2):
-                    c = 2 * (j + PP) + idx
-                    p = 2 * (j - 1) + idx
-                    q = 2 * (j + PP - 1) + idx
-                    has_a = c < NBLK
-                    has_f = 0 <= p < NBLK
-                    if q < NBLK:
-                        quant(q)
-                    if has_a:
-                        a_bank(c, 0)
-                        a_bank(c, 1)
-                    if has_f:
-                        f_bank(p, 0)
-                    if has_a:
-                        a_bank(c, 2)
-                    if has_f:
-                        f_bank(p, 1)
-                    if has_a:
-                        a_bank(c, 3)
-                    if has_f:
-                        f_bank(p, 2)
-                        merges(p)
+                                tail = gi == len(GROUPS) - 1
+                                group_ln(gi, nc.vector if tail else nc.gpsimd)
+                                if tail:
+                                    finish(GROUPS[gi][0], GROUPS[gi][1], nc.vector, nc.sync)
+                                else:
+                                    pending.extend(range(GROUPS[gi][0], GROUPS[gi][1], 2))
+                    if j < NPAIR:
+                        for d in (3, 4, 5):
+                            mx(p0, d)
+                            mx(p1, d)
+                banks = [(b, k) for b in a_list[half] for k in range(4)]
+                if f_list:
+                    f_bank(f_list[half], 0)
+                    f_bank(f_list[half], 1)
+                for b, k in banks:
+                    a_block(b, [k])
+                for b in q_list[half]:
+                    quant(b, 0)
+                    quant(b, 1)
+                if f_list:
+                    t_max(f_list[half])
+                    if half == 1:
+                        bias_add(j - 1, nc.gpsimd)
+                if finished < len(pending):
+                    finish(pending[finished], pending[finished] + 2, nc.gpsimd, nc.gpsimd)
+                    finished += 1

@@ -32,6 +32,9 @@ NEG_BIG = -3.0e38
 W_ENG = ("sv", "sv", "sv", "sv", "sv", "sv")
 EARLY_N = (2, 2, 3, 3, 3, 3)
 EARLY_ENG = ("s", "s", "s", "s", "s", "s")
+PHASES = 4
+V_PHASE = 1
+E_PHASE = 2
 
 
 def tile_compositionalphoneticsmodel_t_kernel(tc, enc_output, feature2phone, mapping, out):
@@ -381,51 +384,59 @@ def tile_compositionalphoneticsmodel_t_kernel(tc, enc_output, feature2phone, map
             p0, p1 = 2 * j, 2 * j + 1
             n0, n1 = p0 + 2, p1 + 2
             if j == 0:
-                a_list = [[4, 5], [6, 7]]
-                q_list = [[], [4, 5]]
+                a_list = [4, 5, 6, 7]
+                q_list = []
             else:
-                a_list = [[b] if b < NBLK else [] for b in (p0 + 2 * AHEAD, p1 + 2 * AHEAD)]
-                q_list = [[b] if b < NBLK else [] for b in (p0 + 2 * AHEAD - 2, p1 + 2 * AHEAD - 2)]
+                a_list = [b for b in (p0 + 2 * AHEAD, p1 + 2 * AHEAD) if b < NBLK]
+                q_list = [b for b in (p0 + 2 * AHEAD - 2, p1 + 2 * AHEAD - 2) if b < NBLK]
             f_list = [p0 - 2, p1 - 2] if 1 <= j <= NPAIR else []
-            for half in range(2):
-                if half == 0:
-                    if j < NPAIR:
-                        for d in (1, 2):
-                            mx(p0, d)
-                            mx(p1, d)
-                    if n0 < NBLK:
-                        mx(n0, 0)
-                        mx(n1, 0)
-                    if j >= 2:
-                        v_max(j - 2)
-                else:
-                    if j >= 2:
-                        exps(j - 2)
-                        for gi in range(len(GROUPS)):
-                            if GROUPS[gi][1] == 2 * (j - 1):
-                                tail = gi == len(GROUPS) - 1
-                                group_ln(gi, nc.vector if tail else nc.gpsimd)
-                                if tail:
-                                    finish(GROUPS[gi][0], GROUPS[gi][1], nc.vector, nc.sync)
-                                else:
-                                    pending.extend(range(GROUPS[gi][0], GROUPS[gi][1], 2))
-                    if j < NPAIR:
-                        for d in (3, 4, 5):
-                            mx(p0, d)
-                            mx(p1, d)
-                banks = [(b, k) for b in a_list[half] for k in range(4)]
-                if f_list:
-                    f_bank(f_list[half], 0)
-                    f_bank(f_list[half], 1)
-                for b, k in banks:
-                    a_block(b, [k])
-                for b in q_list[half]:
-                    quant(b, 0)
-                    quant(b, 1)
-                if f_list:
-                    t_max(f_list[half])
-                    if half == 1:
-                        bias_add(j - 1, nc.gpsimd)
-                if finished < len(pending):
+            m_banks = []
+            if j < NPAIR:
+                m_banks += [(p0, 1), (p1, 1), (p0, 2), (p1, 2)]
+            if n0 < NBLK:
+                m_banks += [(n0, 0), (n1, 0)]
+            if j < NPAIR:
+                m_banks += [(p0, 3), (p1, 3), (p0, 4), (p1, 4), (p0, 5), (p1, 5)]
+            a_banks = [("a", b, k) for b in a_list for k in range(4)]
+            na = len(a_banks) // 2
+            t_banks = []
+            if f_list:
+                t_banks += [("f", f_list[0], 0), ("f", f_list[0], 1)]
+            t_banks += a_banks[:na]
+            if f_list:
+                t_banks += [("f", f_list[1], 0), ("f", f_list[1], 1)]
+            t_banks += a_banks[na:]
+            quants = [(b, g) for b in q_list for g in range(2)]
+            for ph in range(PHASES):
+                for b, d in m_banks[len(m_banks) * ph // PHASES : len(m_banks) * (ph + 1) // PHASES]:
+                    mx(b, d)
+                if ph == V_PHASE and j >= 2:
+                    v_max(j - 2)
+                if ph == E_PHASE and j >= 2:
+                    exps(j - 2)
+                    for gi in range(len(GROUPS)):
+                        if GROUPS[gi][1] == 2 * (j - 1):
+                            tail = gi == len(GROUPS) - 1
+                            group_ln(gi, nc.vector if tail else nc.gpsimd)
+                            if tail:
+                                finish(GROUPS[gi][0], GROUPS[gi][1], nc.vector, nc.sync)
+                            else:
+                                pending.extend(range(GROUPS[gi][0], GROUPS[gi][1], 2))
+                for kind, b, k in t_banks[len(t_banks) * ph // PHASES : len(t_banks) * (ph + 1) // PHASES]:
+                    if kind == "a":
+                        a_block(b, [k])
+                    else:
+                        f_bank(b, k)
+                        if k == 1:
+                            t_max(b)
+                            if b % 2 == 1:
+                                bias_add(b // 2, nc.gpsimd)
+                for b, g in quants[len(quants) * ph // PHASES : len(quants) * (ph + 1) // PHASES]:
+                    quant(b, g)
+                if ph % 2 == 1 and finished < len(pending):
                     finish(pending[finished], pending[finished] + 2, nc.gpsimd, nc.gpsimd)
                     finished += 1
+            if j == 0:
+                for b in (4, 5):
+                    quant(b, 0)
+                    quant(b, 1)

@@ -27,14 +27,15 @@ DEPTH = 6
 NV = 2
 SLOTS = DEPTH * P
 AHEAD = 3
-GROUPS = ((0, 12), (12, 22), (22, 28), (28, 32))
+GROUPS = ((0, 12), (12, 20), (20, 26), (26, 32))
 NEG_BIG = -3.0e38
 W_ENG = ("sv", "sv", "sv", "sv", "sv", "sv")
 EARLY_N = (2, 2, 3, 3, 3, 3)
 EARLY_ENG = ("s", "s", "s", "s", "s", "s")
 PHASES = 4
 V_PHASE = 1
-E_PHASE = 2
+E_PHASE = 3
+SEED_POS = 4
 
 
 def tile_compositionalphoneticsmodel_t_kernel(tc, enc_output, feature2phone, mapping, out):
@@ -303,23 +304,24 @@ def tile_compositionalphoneticsmodel_t_kernel(tc, enc_output, feature2phone, map
                 tps[b // 2] = tp
             nc.vector.tensor_tensor(out=tps[b // 2][:, b % 2, :, :].rearrange("p s c -> p (s c)"), in0=pfs[(b, 1)][:], in1=c0s[b][:], op=ALU.max)
 
-        def bias_add(j, eng):
-            t3 = spool.tile([P, 8, PHONEMES], F32)
-            t3s[j] = t3
+        def bias_add(j, eng, lo=0, hi=8):
+            if lo == 0:
+                t3 = spool.tile([P, 8, PHONEMES], F32)
+                t3s[j] = t3
             eng.tensor_tensor(
-                out=t3[:],
-                in0=tps[j][:].rearrange("p b s c -> p (b s) c")[:, :, 64:128],
-                in1=bias[:].unsqueeze(1).to_broadcast([P, 8, PHONEMES]),
+                out=t3s[j][:, lo:hi, :],
+                in0=tps[j][:].rearrange("p b s c -> p (b s) c")[:, lo:hi, 64:128],
+                in1=bias[:].unsqueeze(1).to_broadcast([P, hi - lo, PHONEMES]),
                 op=ALU.add,
             )
 
-        def v_max(j):
-            vv = v_all[:, j * 512 : (j + 1) * 512].rearrange("p (s m) -> p s m", m=PHONEMES)
-            nc.vector.tensor_tensor(out=vv, in0=tps[j][:].rearrange("p b s c -> p (b s) c")[:, :, 0:64], in1=t3s[j][:], op=ALU.max)
-            nc.vector.tensor_reduce(out=neg_max[:, j * 8 : (j + 1) * 8], in_=vv, axis=AX.X, op=ALU.max, negate=True)
+        def v_max(j, lo=0, hi=8):
+            vv = v_all[:, j * 512 + lo * 64 : j * 512 + hi * 64].rearrange("p (s m) -> p s m", m=PHONEMES)
+            nc.vector.tensor_tensor(out=vv, in0=tps[j][:].rearrange("p b s c -> p (b s) c")[:, lo:hi, 0:64], in1=t3s[j][:, lo:hi, :], op=ALU.max)
+            nc.vector.tensor_reduce(out=neg_max[:, j * 8 + lo : j * 8 + hi], in_=vv, axis=AX.X, op=ALU.max, negate=True)
 
-        def exps(j):
-            for i in range(j * 8, j * 8 + 8):
+        def exps(j, lo=0, hi=8):
+            for i in range(j * 8 + lo, j * 8 + hi):
                 ex = spool.tile([P, PHONEMES], F32)
                 nc.scalar.activation(
                     out=ex[:], in_=v_all[:, i * 64 : (i + 1) * 64], func=ACT.Exp,
@@ -338,6 +340,11 @@ def tile_compositionalphoneticsmodel_t_kernel(tc, enc_output, feature2phone, map
             vg3 = vg.rearrange("p (i m) -> p i m", m=PHONEMES)
             eng.tensor_tensor(out=vg3, in0=vg3, in1=neg_l[:, b0 * 4 : b1 * 4].unsqueeze(2).to_broadcast([P, n, PHONEMES]), op=ALU.add)
             queue.dma_start(out=out_v[:, b0:b1, :], in_=vg.rearrange("p (n f) -> p n f", f=256))
+
+        def finish_scalar(b0, b1, queue):
+            for i in range(b0 * 4, b1 * 4):
+                nc.scalar.activation(out=v_all[:, i * 64 : (i + 1) * 64], in_=v_all[:, i * 64 : (i + 1) * 64], func=ACT.Identity, bias=neg_l[:, i : i + 1], scale=1.0)
+            queue.dma_start(out=out_v[:, b0:b1, :], in_=v_all[:, b0 * 256 : b1 * 256].rearrange("p (n f) -> p n f", f=256))
 
         def a_block(b, ks, engine="s"):
             for k in ks:
@@ -380,7 +387,7 @@ def tile_compositionalphoneticsmodel_t_kernel(tc, enc_output, feature2phone, map
 
         pending = []
         finished = 0
-        for j in range(NPAIR + 2):
+        for j in range(NPAIR):
             p0, p1 = 2 * j, 2 * j + 1
             n0, n1 = p0 + 2, p1 + 2
             if j == 0:
@@ -392,11 +399,9 @@ def tile_compositionalphoneticsmodel_t_kernel(tc, enc_output, feature2phone, map
             f_list = [p0 - 2, p1 - 2] if 1 <= j <= NPAIR else []
             m_banks = []
             if j < NPAIR:
-                m_banks += [(p0, 1), (p1, 1), (p0, 2), (p1, 2)]
+                m_banks += [(b, d) for d in range(1, DEPTH) for b in (p0, p1)]
             if n0 < NBLK:
-                m_banks += [(n0, 0), (n1, 0)]
-            if j < NPAIR:
-                m_banks += [(p0, 3), (p1, 3), (p0, 4), (p1, 4), (p0, 5), (p1, 5)]
+                m_banks = m_banks[:SEED_POS] + [(n0, 0), (n1, 0)] + m_banks[SEED_POS:]
             a_banks = [("a", b, k) for b in a_list for k in range(4)]
             na = len(a_banks) // 2
             t_banks = []
@@ -416,13 +421,10 @@ def tile_compositionalphoneticsmodel_t_kernel(tc, enc_output, feature2phone, map
                     exps(j - 2)
                     for gi in range(len(GROUPS)):
                         if GROUPS[gi][1] == 2 * (j - 1):
-                            tail = gi == len(GROUPS) - 1
-                            group_ln(gi, nc.vector if tail else nc.gpsimd)
-                            if tail:
-                                finish(GROUPS[gi][0], GROUPS[gi][1], nc.vector, nc.sync)
-                            else:
-                                pending.extend(range(GROUPS[gi][0], GROUPS[gi][1], 2))
-                for kind, b, k in t_banks[len(t_banks) * ph // PHASES : len(t_banks) * (ph + 1) // PHASES]:
+                            group_ln(gi, nc.gpsimd)
+                            pending.extend(range(GROUPS[gi][0], GROUPS[gi][1], 2))
+                tp_n = 2 if j == NPAIR - 1 else PHASES
+                for kind, b, k in t_banks[len(t_banks) * min(ph, tp_n) // tp_n : len(t_banks) * min(ph + 1, tp_n) // tp_n]:
                     if kind == "a":
                         a_block(b, [k])
                     else:
@@ -440,3 +442,24 @@ def tile_compositionalphoneticsmodel_t_kernel(tc, enc_output, feature2phone, map
                 for b in (4, 5):
                     quant(b, 0)
                     quant(b, 1)
+
+        assert finished == len(pending)
+        z = NPAIR - 1
+        v_max(z - 1)
+        f_bank(2 * z, 0)
+        f_bank(2 * z, 1)
+        f_bank(2 * z + 1, 0)
+        exps(z - 1)
+        for b in (2 * z, 2 * z + 1):
+            lo = 4 * (b % 2)
+            t_max(b)
+            if b == 2 * z:
+                f_bank(b + 1, 1)
+            bias_add(z, nc.vector, lo, lo + 4)
+            v_max(z, lo, lo + 4)
+            exps(z, lo, lo + 4)
+        g0 = GROUPS[-1][0]
+        group_ln(len(GROUPS) - 1, nc.vector)
+        finish(g0, g0 + 2, nc.vector, nc.sync)
+        finish_scalar(g0 + 2, g0 + 4, nc.scalar)
+        finish(g0 + 4, NBLK, nc.vector, nc.sync)

@@ -234,7 +234,10 @@ def tile_compositionalphoneticsmodel_t_kernel(tc, enc_output, feature2phone, map
         logs = const.tile([P, NBLK * 4], F32)
         neg_l = const.tile([P, NBLK * 4], F32)
 
-        def a_bank(b, k, engine="s"):
+        def bridge(bank):
+            nc.tensor.matmul(out=bank[:, 0:32], lhsT=ones[:], rhs=ones[:, 0:32], start=True, stop=True)
+
+        def a_bank(b, k, engine="s", first=False):
             if k == 0:
                 gr = gpool.tile([P, 2 * BLOCK * 4], BF16, align_bytes=64)
                 grs[b] = gr
@@ -243,6 +246,8 @@ def tile_compositionalphoneticsmodel_t_kernel(tc, enc_output, feature2phone, map
             xw = xs[b][:].bitcast(F32)
             grw = grs[b][:].bitcast(F32)
             pt = ps_t.tile([P, 4 * P], F32, tag="pt")
+            if first:
+                bridge(pt)
             for u in range(2):
                 for s2 in range(2):
                     col = (2 * sp + s2) * 512 + 256 * g + 128 * u
@@ -267,12 +272,14 @@ def tile_compositionalphoneticsmodel_t_kernel(tc, enc_output, feature2phone, map
                 in_=grs[b][:, g * BLOCK * 4 : (g + 1) * BLOCK * 4],
             )
 
-        def mx(b, d):
+        def mx(b, d, first=False):
             if d == 0:
                 acc = apool.tile([P, BLOCK], F32)
                 accs[b] = acc
             codes, scales = cds[b]
             pm = ps_m.tile([P, BLOCK], F32, tag="pm")
+            if first:
+                bridge(pm)
             for g in range(2):
                 nc.tensor.matmul_mx(
                     out=pm[:],
@@ -288,8 +295,10 @@ def tile_compositionalphoneticsmodel_t_kernel(tc, enc_output, feature2phone, map
             else:
                 nc.vector.scalar_tensor_tensor(out=accs[b][:], in0=pm[:], scalar=gain[:, d : d + 1], in1=accs[b][:], op0=ALU.mult, op1=ALU.max)
 
-        def f_bank(b, h):
+        def f_bank(b, h, first=False):
             pf = ps_f.tile([P, 4 * P], F32, tag="pf%d" % h, name="pf%d" % h)
+            if first:
+                bridge(pf)
             for s in range(4):
                 nc.tensor.transpose(pf[:, s * P : (s + 1) * P], accs[b][:, s * P : (s + 1) * P], perm2[:, h * P : (h + 1) * P])
             pfs[(b, h)] = pf
@@ -346,9 +355,9 @@ def tile_compositionalphoneticsmodel_t_kernel(tc, enc_output, feature2phone, map
                 nc.scalar.activation(out=v_all[:, i * 64 : (i + 1) * 64], in_=v_all[:, i * 64 : (i + 1) * 64], func=ACT.Identity, bias=neg_l[:, i : i + 1], scale=1.0)
             queue.dma_start(out=out_v[:, b0:b1, :], in_=v_all[:, b0 * 256 : b1 * 256].rearrange("p (n f) -> p n f", f=256))
 
-        def a_block(b, ks, engine="s"):
+        def a_block(b, ks, engine="s", first=False):
             for k in ks:
-                a_bank(b, k, engine)
+                a_bank(b, k, engine, first)
                 if k == 3 and b + 4 < NBLK:
                     load(b + 4)
 
@@ -413,8 +422,8 @@ def tile_compositionalphoneticsmodel_t_kernel(tc, enc_output, feature2phone, map
             t_banks += a_banks[na:]
             quants = [(b, g) for b in q_list for g in range(2)]
             for ph in range(PHASES):
-                for b, d in m_banks[len(m_banks) * ph // PHASES : len(m_banks) * (ph + 1) // PHASES]:
-                    mx(b, d)
+                for n, (b, d) in enumerate(m_banks[len(m_banks) * ph // PHASES : len(m_banks) * (ph + 1) // PHASES]):
+                    mx(b, d, n == 0)
                 if ph == V_PHASE and j >= 2:
                     v_max(j - 2)
                 if ph == E_PHASE and j >= 2:
@@ -424,11 +433,11 @@ def tile_compositionalphoneticsmodel_t_kernel(tc, enc_output, feature2phone, map
                             group_ln(gi, nc.gpsimd)
                             pending.extend(range(GROUPS[gi][0], GROUPS[gi][1], 2))
                 tp_n = 2 if j == NPAIR - 1 else PHASES
-                for kind, b, k in t_banks[len(t_banks) * min(ph, tp_n) // tp_n : len(t_banks) * min(ph + 1, tp_n) // tp_n]:
+                for n, (kind, b, k) in enumerate(t_banks[len(t_banks) * min(ph, tp_n) // tp_n : len(t_banks) * min(ph + 1, tp_n) // tp_n]):
                     if kind == "a":
-                        a_block(b, [k])
+                        a_block(b, [k], "s", n == 0)
                     else:
-                        f_bank(b, k)
+                        f_bank(b, k, n == 0)
                         if k == 1:
                             t_max(b)
                             if b % 2 == 1:
@@ -446,7 +455,7 @@ def tile_compositionalphoneticsmodel_t_kernel(tc, enc_output, feature2phone, map
         assert finished == len(pending)
         z = NPAIR - 1
         v_max(z - 1)
-        f_bank(2 * z, 0)
+        f_bank(2 * z, 0, True)
         f_bank(2 * z, 1)
         f_bank(2 * z + 1, 0)
         exps(z - 1)

from contextlib import ExitStack

import concourse.mybir as mybir
from concourse.masks import make_identity

F32 = mybir.dt.float32
BF16 = mybir.dt.bfloat16
I32 = mybir.dt.int32
U32 = mybir.dt.uint32
U8 = mybir.dt.uint8
FP8X4 = mybir.dt.float8_e4m3fn_x4
ALU = mybir.AluOpType
ACT = mybir.ActivationFunctionType
AX = mybir.AxisListType

TOKENS = 16 * 1024
H = 1024
PHONES = 256
PHONEMES = 64
FLOPS = 2 * TOKENS * H * PHONES

P = 128
BLOCK = 512
NBLK = TOKENS // BLOCK
NPAIR = NBLK // 2
DEPTH = 6
NV = 2
SLOTS = DEPTH * P
AHEAD = 3
GROUPS = ((0, 12), (12, 20), (20, 26), (26, 32))
NEG_BIG = -3.0e38
W_ENG = ("sv", "sv", "sv", "sv", "sv", "sv")
EARLY_N = (2, 2, 3, 3, 3, 3)
EARLY_ENG = ("s", "s", "s", "s", "s", "s")
PHASES = 4
V_PHASE = 1
E_PHASE = 3
SEED_POS = 4


def tile_compositionalphoneticsmodel_t_kernel(tc, enc_output, feature2phone, mapping, out):
    nc = tc.nc
    enc_v = enc_output.rearrange("b t k -> (b t) k").rearrange("(n p s) k -> n p (s k)", p=P, s=4)
    out_v = out.rearrange("b t m -> (b t) m").rearrange("(n p s) m -> p n (s m)", p=P, s=4)
    w_v = feature2phone.rearrange("(a q e) p -> e q a p", a=4, q=P, e=2)

    with ExitStack() as ctx:
        const = ctx.enter_context(tc.tile_pool(name="const", bufs=1))
        xpool = ctx.enter_context(tc.tile_pool(name="xpool", bufs=4))
        gpool = ctx.enter_context(tc.tile_pool(name="gpool", bufs=4))
        cpool = ctx.enter_context(tc.tile_pool(name="cpool", bufs=8))
        apool = ctx.enter_context(tc.tile_pool(name="apool", bufs=6))
        spool = ctx.enter_context(tc.tile_pool(name="spool", bufs=2))
        ps_t = ctx.enter_context(tc.psum_pool(name="ps_t", bufs=3))
        ps_m = ctx.enter_context(tc.psum_pool(name="ps_m", bufs=3))
        ps_f = ctx.enter_context(tc.psum_pool(name="ps_f", bufs=1))
        ctx.enter_context(tc.manual_schedule())

        xs = {}
        grs = {}
        cds = {}
        accs = {}
        pfs = {}
        c0s = {}
        tps = {}
        t3s = {}

        map2 = const.tile([P, PHONES], BF16)
        nc.sync.dma_start(out=map2[0:64, :], in_=mapping)
        nc.sync.dma_start(out=map2[64:128, :], in_=mapping)
        wl = const.tile([P, 4, 2, PHONES], BF16)
        for e in range(2):
            nc.sync.dma_start(out=wl[:, :, e, :], in_=w_v[e])

        def load(b):
            x = xpool.tile([P, 4 * H], BF16)
            nc.sync.dma_start(out=x[:], in_=enc_v[b])
            xs[b] = x

        for b in range(4):
            load(b)

        part_i = const.tile([P, 1], I32)
        nc.gpsimd.iota(part_i[:], pattern=[[0, 1]], base=0, channel_multiplier=1)
        slot_i = const.tile([P, NV * DEPTH], I32)
        nc.gpsimd.iota(slot_i[:], pattern=[[2 * DEPTH, NV], [1, DEPTH]], base=0, channel_multiplier=0)
        iota_i = const.tile([P, P], I32)
        nc.gpsimd.iota(iota_i[:], pattern=[[1, P]], base=0, channel_multiplier=0)
        ident_b = const.tile([P, P], BF16)
        make_identity(nc, ident_b[:])
        ident_f = const.tile([P, P], F32)
        make_identity(nc, ident_f[:])

        part_f = const.tile([P, 1], F32)
        nc.vector.tensor_copy(out=part_f[:], in_=part_i[:])
        slot_f = const.tile([P, NV * DEPTH], F32)
        nc.vector.tensor_copy(out=slot_f[:], in_=slot_i[:])
        half_d = const.tile([P, 1], F32)
        nc.vector.tensor_scalar(out=half_d[:], in0=part_f[:], scalar1=64.0, scalar2=float(DEPTH), op0=ALU.is_ge, op1=ALU.mult)
        want0 = const.tile([P, NV * DEPTH], F32)
        nc.vector.tensor_scalar(out=want0[:], in0=slot_f[:], scalar1=half_d[:, 0:1], scalar2=None, op0=ALU.add)
        iota_f = const.tile([P, P], F32)
        nc.vector.tensor_copy(out=iota_f[:], in_=iota_i[:])
        tri = const.tile([P, P], BF16)
        nc.vector.tensor_scalar(out=tri[:], in0=iota_f[:], scalar1=part_f[:, 0:1], scalar2=None, op0=ALU.is_gt)
        ones = const.tile([P, P], BF16)
        nc.vector.memset(ones[:], 1.0)
        gain_b = const.tile([P, NV, 32], BF16)
        nc.vector.memset(gain_b[:], 0.0)

        mask = const.tile([P, PHONES], F32)
        nc.vector.tensor_single_scalar(out=mask[:], in_=map2[:], scalar=0.0, op=ALU.is_gt)
        incl = const.tile([P, PHONES], F32)
        nc.vector.tensor_tensor_scan(out=incl[:], data0=mask[:], data1=mask[:], initial=0.0, op0=ALU.add, op1=ALU.max)
        rank1 = const.tile([P, PHONES], F32)
        nc.vector.tensor_tensor(out=rank1[:], in0=incl[:], in1=mask[:], op=ALU.mult)
        count = incl[:, PHONES - 1 : PHONES]
        valid = const.tile([P, NV * DEPTH], F32)
        nc.vector.tensor_scalar(out=valid[:], in0=want0[:], scalar1=count, scalar2=None, op0=ALU.is_lt)
        valid_v = valid[:].rearrange("v (h d) -> v h d", d=DEPTH)
        active = valid_v[:, :, 0]
        act_b = const.tile([P, NV, 32], BF16)
        nc.vector.tensor_copy(out=act_b[:], in_=valid_v[:, :, 0:1].to_broadcast([P, NV, 32]))
        want_t = const.tile([P, NV * DEPTH], F32)
        nc.vector.tensor_tensor(out=want_t[:], in0=want0[:], in1=valid[:], op=ALU.mult)
        want1 = const.tile([P, NV * DEPTH], F32)
        nc.vector.tensor_single_scalar(out=want1[:], in_=want_t[:], scalar=1.0, op=ALU.add)

        lid_p = ps_m.tile([P, NV, 32], F32, tag="pm")
        nc.tensor.matmul(out=lid_p[:, 0, :], lhsT=tri[:], rhs=act_b[:, 0, :], start=True, stop=True)
        nc.tensor.matmul(out=lid_p[:, 1, :], lhsT=ones[:], rhs=act_b[:, 0, :], start=True, stop=False)
        nc.tensor.matmul(out=lid_p[:, 1, :], lhsT=tri[:], rhs=act_b[:, 1, :], start=False, stop=True)

        sgw = const.tile([P, NV * DEPTH, PHONES], BF16)
        gain_v = const.tile([P, NV * DEPTH], F32)

        def sgw_make(d):
            for h in range(NV):
                j = h * DEPTH + d
                nc.vector.scalar_tensor_tensor(
                    out=sgw[:, j, :], in0=rank1[:], scalar=want1[:, j : j + 1], in1=map2[:],
                    op0=ALU.is_equal, op1=ALU.mult, accum_out=gain_v[:, j : j + 1],
                )

        sgw_make(0)

        lid_t = const.tile([P, NV], F32)
        nc.vector.scalar_tensor_tensor(out=lid_t[:], in0=lid_p[:, :, 0], scalar=1.0, in1=active, op0=ALU.add, op1=ALU.mult)
        lane_id = const.tile([P, NV], F32)
        nc.vector.tensor_single_scalar(out=lane_id[:], in_=lid_t[:], scalar=-1.0, op=ALU.add)
        compact = const.tile([P, NV, P], BF16)
        for h in range(NV):
            nc.vector.tensor_scalar(out=compact[:, h, :], in0=iota_f[:], scalar1=lane_id[:, h : h + 1], scalar2=None, op0=ALU.is_equal)
        tg1 = const.tile([P, 1], F32)
        nc.vector.scalar_tensor_tensor(out=tg1[:], in0=lid_p[:, 1, 0:1], scalar=lane_id[:, 0:1], in1=valid_v[:, 1, 0:1], op0=ALU.subtract, op1=ALU.mult)
        tgt_b = const.tile([P, NV], BF16)
        nc.vector.tensor_copy(out=tgt_b[:, 0:1], in_=lane_id[:, 0:1])
        nc.vector.tensor_scalar(out=tgt_b[:, 1:2], in0=tg1[:], scalar1=lane_id[:, 0:1], scalar2=None, op0=ALU.add)

        wt = []

        def wt_make(c):
            wt_p = ps_t.tile([P, 8 * P], BF16, tag="pt")
            for a in range(4):
                for e in range(2):
                    nc.tensor.transpose(wt_p[:, (a * 2 + e) * P : (a * 2 + e + 1) * P], wl[:, a, e, c * P : (c + 1) * P], ident_b[:])
            wt_c = const.tile([P, 8 * P], BF16, name="wt%d" % c)
            nc.scalar.copy(out=wt_c[:], in_=wt_p[:])
            wt.append(wt_c)

        sel = const.tile([P, DEPTH, 2, P], BF16)

        def sel_make(d):
            sel_p = ps_f.tile([P, 2, P], F32, tag="pf%d" % (d % 2), name="sel_p")
            for c in range(2):
                for h in range(NV):
                    nc.tensor.matmul(
                        out=sel_p[:, c, :],
                        lhsT=sgw[:, h * DEPTH + d, c * P : (c + 1) * P],
                        rhs=compact[:, h, :],
                        start=(h == 0),
                        stop=(h == NV - 1),
                    )
            nc.scalar.activation(out=sel[:, d, :, :], in_=sel_p[:], func=ACT.Sign)

        wg = const.tile([P, 2, DEPTH, P * 4], BF16, align_bytes=64)
        w_codes = const.tile([P, 2, DEPTH, P], U32, align_bytes=64)
        w_scales = const.tile([P, 2, DEPTH, P], U8, align_bytes=64)

        def wslot_make(d, engines):
            for g in range(2):
                wp = ps_m.tile([P, 4 * P], F32, tag="pm")
                for ue in range(4):
                    for c in range(2):
                        nc.tensor.matmul(
                            out=wp[:, ue * P : (ue + 1) * P],
                            lhsT=wt[c][:, (g * 4 + ue) * P : (g * 4 + ue + 1) * P],
                            rhs=sel[:, d, c, :],
                            start=(c == 0),
                            stop=(c == 1),
                        )
                dst = wg[:, g, d, :].rearrange("q (l t) -> q l t", t=4)
                src = wp[:].rearrange("q (t l) -> q l t", t=4)
                if engines[g] == "v":
                    nc.vector.tensor_copy(out=dst, in_=src)
                else:
                    nc.scalar.copy(out=dst, in_=src)

        def wslot_quant(d):
            for g in range(2):
                nc.vector.quantize_mx(out=w_codes[:, g, d, :].bitcast(FP8X4), scales=w_scales[:, g, d, :], in_=wg[:, g, d, :])

        gain = const.tile([P, DEPTH], F32)
        perm2 = const.tile([P, NV * P], F32)
        bias = const.tile([P, PHONEMES], F32)

        def gain_make():
            nc.vector.tensor_copy(out=gain_b[:, :, 0:DEPTH], in_=gain_v[:].rearrange("v (h d) -> v h d", d=DEPTH))
            gain_p = ps_f.tile([P, 32], F32, tag="pf0")
            for h in range(NV):
                nc.tensor.matmul(out=gain_p[:], lhsT=compact[:, h, :], rhs=gain_b[:, h, :], start=(h == 0), stop=(h == NV - 1))
            nc.vector.tensor_single_scalar(out=gain[:], in_=gain_p[:, 0:DEPTH], scalar=1.0 / 32.0, op=ALU.mult)

        def perm_make():
            row_p = ps_f.tile([P, NV * P], F32, tag="pf1")
            for h in range(NV):
                nc.tensor.matmul(out=row_p[:, h * P : (h + 1) * P], lhsT=tgt_b[:, h : h + 1].to_broadcast([P, P]), rhs=ident_b[:], start=True, stop=True)
            nc.vector.tensor_scalar(out=perm2[:], in0=row_p[:], scalar1=part_f[:, 0:1], scalar2=None, op0=ALU.is_equal)
            nc.vector.tensor_scalar(out=bias[:], in0=row_p[:, 64:128], scalar1=0.0, scalar2=NEG_BIG, op0=ALU.is_lt, op1=ALU.mult)

        v_all = const.tile([P, NBLK * 256], F32)
        neg_max = const.tile([P, NBLK * 4], F32)
        sums = const.tile([P, NBLK * 4], F32)
        logs = const.tile([P, NBLK * 4], F32)
        neg_l = const.tile([P, NBLK * 4], F32)

        def bridge(bank):
            nc.tensor.matmul(out=bank[:, 0:32], lhsT=ones[:], rhs=ones[:, 0:32], start=True, stop=True)

        def a_bank(b, k, engine="s", first=False):
            if k == 0:
                gr = gpool.tile([P, 2 * BLOCK * 4], BF16, align_bytes=64)
                grs[b] = gr
            g = k // 2
            sp = k % 2
            xw = xs[b][:].bitcast(F32)
            grw = grs[b][:].bitcast(F32)
            pt = ps_t.tile([P, 4 * P], F32, tag="pt")
            if first:
                bridge(pt)
            for u in range(2):
                for s2 in range(2):
                    col = (2 * sp + s2) * 512 + 256 * g + 128 * u
                    nc.tensor.transpose(pt[:, (u * 2 + s2) * P : (u * 2 + s2 + 1) * P], xw[:, col : col + P], ident_f[:])
            lo = g * 1024 + sp * 512
            dst = grw[:, lo : lo + 512].rearrange("q (t u) -> q t u", u=2)
            src = pt[:].rearrange("q (u t) -> q t u", u=2)
            if engine == "v":
                nc.vector.tensor_copy(out=dst, in_=src)
            else:
                nc.scalar.copy(out=dst, in_=src)

        def quant(b, g):
            if g == 0:
                codes = cpool.tile([P, 2 * BLOCK], U32, align_bytes=64)
                scales = cpool.tile([P, 2 * BLOCK], U8, align_bytes=64)
                cds[b] = (codes, scales)
            codes, scales = cds[b]
            nc.vector.quantize_mx(
                out=codes[:, g * BLOCK : (g + 1) * BLOCK].bitcast(FP8X4),
                scales=scales[:, g * BLOCK : (g + 1) * BLOCK],
                in_=grs[b][:, g * BLOCK * 4 : (g + 1) * BLOCK * 4],
            )

        def mx(b, d, first=False):
            if d == 0:
                acc = apool.tile([P, BLOCK], F32)
                accs[b] = acc
            codes, scales = cds[b]
            pm = ps_m.tile([P, BLOCK], F32, tag="pm")
            if first:
                bridge(pm)
            for g in range(2):
                nc.tensor.matmul_mx(
                    out=pm[:],
                    lhsT=w_codes[:, g, d, :].bitcast(FP8X4),
                    lhsT_scale=w_scales[:, g, d, :],
                    rhs=codes[:, g * BLOCK : (g + 1) * BLOCK].bitcast(FP8X4),
                    rhs_scale=scales[:, g * BLOCK : (g + 1) * BLOCK],
                    start=(g == 0),
                    stop=(g == 1),
                )
            if d == 0:
                nc.scalar.activation(out=accs[b][:], in_=pm[:], func=ACT.Copy, scale=gain[:, 0:1])
            else:
                nc.vector.scalar_tensor_tensor(out=accs[b][:], in0=pm[:], scalar=gain[:, d : d + 1], in1=accs[b][:], op0=ALU.mult, op1=ALU.max)

        def f_bank(b, h, first=False):
            pf = ps_f.tile([P, 4 * P], F32, tag="pf%d" % h, name="pf%d" % h)
            if first:
                bridge(pf)
            for s in range(4):
                nc.tensor.transpose(pf[:, s * P : (s + 1) * P], accs[b][:, s * P : (s + 1) * P], perm2[:, h * P : (h + 1) * P])
            pfs[(b, h)] = pf
            if h == 0:
                c0 = spool.tile([P, 4 * P], F32)
                nc.scalar.copy(out=c0[:], in_=pf[:])
                c0s[b] = c0

        def t_max(b):
            if b % 2 == 0:
                tp = spool.tile([P, 2, 4, P], F32)
                tps[b // 2] = tp
            nc.vector.tensor_tensor(out=tps[b // 2][:, b % 2, :, :].rearrange("p s c -> p (s c)"), in0=pfs[(b, 1)][:], in1=c0s[b][:], op=ALU.max)

        def bias_add(j, eng, lo=0, hi=8):
            if lo == 0:
                t3 = spool.tile([P, 8, PHONEMES], F32)
                t3s[j] = t3
            eng.tensor_tensor(
                out=t3s[j][:, lo:hi, :],
                in0=tps[j][:].rearrange("p b s c -> p (b s) c")[:, lo:hi, 64:128],
                in1=bias[:].unsqueeze(1).to_broadcast([P, hi - lo, PHONEMES]),
                op=ALU.add,
            )

        def v_max(j, lo=0, hi=8):
            vv = v_all[:, j * 512 + lo * 64 : j * 512 + hi * 64].rearrange("p (s m) -> p s m", m=PHONEMES)
            nc.vector.tensor_tensor(out=vv, in0=tps[j][:].rearrange("p b s c -> p (b s) c")[:, lo:hi, 0:64], in1=t3s[j][:, lo:hi, :], op=ALU.max)
            nc.vector.tensor_reduce(out=neg_max[:, j * 8 + lo : j * 8 + hi], in_=vv, axis=AX.X, op=ALU.max, negate=True)

        def exps(j, lo=0, hi=8):
            for i in range(j * 8 + lo, j * 8 + hi):
                ex = spool.tile([P, PHONEMES], F32)
                nc.scalar.activation(
                    out=ex[:], in_=v_all[:, i * 64 : (i + 1) * 64], func=ACT.Exp,
                    bias=neg_max[:, i : i + 1], scale=1.0, accum_out=sums[:, i : i + 1],
                )

        def group_ln(gi, eng):
            g0, g1 = GROUPS[gi]
            cols = slice(g0 * 4, g1 * 4)
            nc.scalar.activation(out=logs[:, cols], in_=sums[:, cols], func=ACT.Ln)
            eng.tensor_tensor(out=neg_l[:, cols], in0=neg_max[:, cols], in1=logs[:, cols], op=ALU.subtract)

        def finish(b0, b1, eng, queue):
            n = (b1 - b0) * 4
            vg = v_all[:, b0 * 256 : b1 * 256]
            vg3 = vg.rearrange("p (i m) -> p i m", m=PHONEMES)
            eng.tensor_tensor(out=vg3, in0=vg3, in1=neg_l[:, b0 * 4 : b1 * 4].unsqueeze(2).to_broadcast([P, n, PHONEMES]), op=ALU.add)
            queue.dma_start(out=out_v[:, b0:b1, :], in_=vg.rearrange("p (n f) -> p n f", f=256))

        def finish_scalar(b0, b1, queue):
            for i in range(b0 * 4, b1 * 4):
                nc.scalar.activation(out=v_all[:, i * 64 : (i + 1) * 64], in_=v_all[:, i * 64 : (i + 1) * 64], func=ACT.Identity, bias=neg_l[:, i : i + 1], scale=1.0)
            queue.dma_start(out=out_v[:, b0:b1, :], in_=v_all[:, b0 * 256 : b1 * 256].rearrange("p (n f) -> p n f", f=256))

        def a_block(b, ks, engine="s", first=False):
            for k in ks:
                a_bank(b, k, engine, first)
                if k == 3 and b + 4 < NBLK:
                    load(b + 4)

        wt_make(0)
        wt_make(1)
        sel_make(0)
        sgw_make(1)
        sel_make(1)
        sgw_make(2)
        early = [(b, k) for b in range(4) for k in range(4)]
        for d in range(DEPTH):
            wslot_make(d, W_ENG[d])
            if d + 2 < DEPTH:
                sel_make(d + 2)
            if d + 3 < DEPTH:
                sgw_make(d + 3)
            for b, k in early[sum(EARLY_N[:d]) : sum(EARLY_N[: d + 1])]:
                a_block(b, [k], EARLY_ENG[d])
            wslot_quant(d)
            if d == 3:
                quant(0, 0)
                quant(0, 1)
            if d == 4:
                gain_make()
                perm_make()
        for b, k in early[sum(EARLY_N) :]:
            a_block(b, [k])
        quant(1, 0)
        quant(1, 1)
        mx(0, 0)
        mx(1, 0)
        quant(2, 0)
        quant(2, 1)
        quant(3, 0)
        quant(3, 1)

        pending = []
        finished = 0
        for j in range(NPAIR):
            p0, p1 = 2 * j, 2 * j + 1
            n0, n1 = p0 + 2, p1 + 2
            if j == 0:
                a_list = [4, 5, 6, 7]
                q_list = []
            else:
                a_list = [b for b in (p0 + 2 * AHEAD, p1 + 2 * AHEAD) if b < NBLK]
                q_list = [b for b in (p0 + 2 * AHEAD - 2, p1 + 2 * AHEAD - 2) if b < NBLK]
            f_list = [p0 - 2, p1 - 2] if 1 <= j <= NPAIR else []
            m_banks = []
            if j < NPAIR:
                m_banks += [(b, d) for d in range(1, DEPTH) for b in (p0, p1)]
            if n0 < NBLK:
                m_banks = m_banks[:SEED_POS] + [(n0, 0), (n1, 0)] + m_banks[SEED_POS:]
            a_banks = [("a", b, k) for b in a_list for k in range(4)]
            na = len(a_banks) // 2
            t_banks = []
            if f_list:
                t_banks += [("f", f_list[0], 0), ("f", f_list[0], 1)]
            t_banks += a_banks[:na]
            if f_list:
                t_banks += [("f", f_list[1], 0), ("f", f_list[1], 1)]
            t_banks += a_banks[na:]
            quants = [(b, g) for b in q_list for g in range(2)]
            for ph in range(PHASES):
                for n, (b, d) in enumerate(m_banks[len(m_banks) * ph // PHASES : len(m_banks) * (ph + 1) // PHASES]):
                    mx(b, d, n == 0)
                if ph == V_PHASE and j >= 2:
                    v_max(j - 2)
                if ph == E_PHASE and j >= 2:
                    exps(j - 2)
                    for gi in range(len(GROUPS)):
                        if GROUPS[gi][1] == 2 * (j - 1):
                            group_ln(gi, nc.gpsimd)
                            pending.extend(range(GROUPS[gi][0], GROUPS[gi][1], 2))
                tp_n = 2 if j == NPAIR - 1 else PHASES
                for n, (kind, b, k) in enumerate(t_banks[len(t_banks) * min(ph, tp_n) // tp_n : len(t_banks) * min(ph + 1, tp_n) // tp_n]):
                    if kind == "a":
                        a_block(b, [k], "s", n == 0)
                    else:
                        f_bank(b, k, n == 0)
                        if k == 1:
                            t_max(b)
                            if b % 2 == 1:
                                bias_add(b // 2, nc.gpsimd)
                for b, g in quants[len(quants) * ph // PHASES : len(quants) * (ph + 1) // PHASES]:
                    quant(b, g)
                if ph % 2 == 1 and finished < len(pending):
                    finish(pending[finished], pending[finished] + 2, nc.gpsimd, nc.gpsimd)
                    finished += 1
            if j == 0:
                for b in (4, 5):
                    quant(b, 0)
                    quant(b, 1)

        assert finished == len(pending)
        z = NPAIR - 1
        v_max(z - 1)
        f_bank(2 * z, 0, True)
        f_bank(2 * z, 1)
        f_bank(2 * z + 1, 0)
        exps(z - 1)
        for b in (2 * z, 2 * z + 1):
            lo = 4 * (b % 2)
            t_max(b)
            if b == 2 * z:
                f_bank(b + 1, 1)
            bias_add(z, nc.vector, lo, lo + 4)
            v_max(z, lo, lo + 4)
            exps(z, lo, lo + 4)
        g0 = GROUPS[-1][0]
        group_ln(len(GROUPS) - 1, nc.vector)
        finish(g0, g0 + 2, nc.vector, nc.sync)
        finish_scalar(g0 + 2, g0 + 4, nc.scalar)
        finish(g0 + 4, NBLK, nc.vector, nc.sync)
